import numpy as np
import ml_dtypes


def mxq(x, axis, fmt="e4m3"):
    dtype, down = {"e4m3": (ml_dtypes.float8_e4m3fn, 7), "e5m2": (ml_dtypes.float8_e5m2, 14)}[fmt]
    v = np.moveaxis(np.asarray(x, np.float32).astype(ml_dtypes.bfloat16).astype(np.float64), axis, -1)
    blocks = v.reshape(v.shape[:-1] + (-1, 32))
    amax = np.abs(blocks).max(-1, keepdims=True)
    byte = np.maximum(np.where(amax > 0, np.frexp(amax)[1] - 1 + 127, 0) - down, 1)
    scale = np.exp2(byte - 127.0)
    codes = (blocks / scale).astype(np.float32).astype(dtype).astype(np.float64)
    return np.moveaxis((codes * scale).reshape(v.shape), -1, axis)


WIDE = False


def mx_kscale(k):
    if not WIDE:
        return np.ones(k)
    levels = np.array([10, -10, 5, -5, 0])
    a = np.random.permutation(np.resize(levels, k // 512 * 4)).reshape(k // 512, 4)
    idx = np.arange(k)
    return np.exp2(a[idx // 512, idx % 128 // 32])


BF16 = ml_dtypes.bfloat16


def bf(x):
    return np.asarray(x, np.float32).astype(BF16)


def f64(x):
    return np.asarray(x).astype(np.float64)


E2M1 = np.array([0.0, 0.5, 1.0, 1.5, 2.0, 3.0, 4.0, 6.0, -0.0, -0.5, -1.0, -1.5, -2.0, -3.0, -4.0, -6.0])


def pack_weight(w, fmt):
    k, n = w.shape
    w = f64(bf(w)).reshape(k // 32, 32, n)
    amax = np.abs(w).max(1)
    if fmt == "e4m3":
        byte = np.frexp(amax)[1] - 1 + 127 - 7
    else:
        mant, ex = np.frexp(amax / 6.0)
        byte = np.where(mant > 0.5, ex, ex - 1) + 127
    byte = np.clip(np.where(amax > 0, byte, 1), 1, 254)
    scaled = (w * np.exp2(127.0 - byte)[:, None, :]).reshape(k, n).astype(np.float32)
    by_word = np.ascontiguousarray(scaled.reshape(k // 512, 128, 4, n).transpose(0, 1, 3, 2))
    if fmt == "e4m3":
        words = by_word.astype(ml_dtypes.float8_e4m3fn).view(np.uint8)
    else:
        c = by_word.astype(ml_dtypes.float4_e2m1fn).view(np.uint8) & 0xF
        words = c[..., 0::2] | (c[..., 1::2] << 4)
    return np.ascontiguousarray(words), np.ascontiguousarray(byte.astype(np.uint8).reshape(k // 512, 16, n))


def unpack_weight(words, scales, fmt):
    g, p, n, _ = words.shape
    if fmt == "e4m3":
        vals = np.ascontiguousarray(words).view(ml_dtypes.float8_e4m3fn).astype(np.float64)
    else:
        nib = np.empty((g, p, n, 4), np.uint8)
        nib[..., 0::2] = words & 0xF
        nib[..., 1::2] = words >> 4
        vals = E2M1[nib]
    vals = vals * np.repeat(np.exp2(scales.astype(np.float64) - 127.0), 8, axis=1)[..., None]
    return vals.transpose(0, 1, 3, 2).reshape(g * 512, n)


B, I, H = 256, 16384, 1024
EPS = 1e-5
FMT = "e4m3"


def ln(v):
    mu = v.mean(-1, keepdims=True)
    var = np.square(v - mu).mean(-1, keepdims=True)
    return (v - mu) / np.sqrt(var + EPS)


def sigmoid(v):
    return 1.0 / (1.0 + np.exp(-v))


def setup_inputs():
    s = mx_kscale(I)
    x = bf(np.random.standard_normal((B, I)) * s)
    h = bf(np.random.standard_normal((B, H)))
    r = bf(sigmoid(np.sqrt(2.0) * np.random.standard_normal((B, H))))
    z = bf(sigmoid(np.sqrt(2.0) * np.random.standard_normal((B, H))))
    W_in = np.random.standard_normal((H, I)) / np.sqrt(I) / s
    b_in = bf(np.random.standard_normal(H) * 0.5)
    W_hn = np.random.standard_normal((H, H)) / np.sqrt(H)
    b_hn = bf(np.random.standard_normal(H) * 0.5)
    W_in_words, W_in_scales = pack_weight(np.ascontiguousarray(W_in.T), FMT)
    W_hn_words, W_hn_scales = pack_weight(np.ascontiguousarray(W_hn.T), FMT)
    return {"x": x,
            "h": h,
            "r": r,
            "z": z,
            "W_in_words": W_in_words,
            "W_in_scales": W_in_scales,
            "b_in": b_in,
            "W_hn_words": W_hn_words,
            "W_hn_scales": W_hn_scales,
            "b_hn": b_hn}


def reference(x, h, r, z, W_in_words, W_in_scales, b_in, W_hn_words, W_hn_scales, b_hn):
    h = f64(h)
    r, z = f64(r), f64(z)
    i_n = ln((mxq(f64(x), 1, "e4m3") @ unpack_weight(W_in_words, W_in_scales, FMT)) + f64(b_in))
    h_n = ln((mxq(h, 1, "e4m3") @ unpack_weight(W_hn_words, W_hn_scales, FMT)) + f64(b_hn))
    n = np.tanh(i_n + r * h_n)
    return (1.0 - z) * n + z * h

@@ -1,0 +1,230 @@
+from contextlib import ExitStack
+
+import concourse.mybir as mybir
+from concourse.masks import make_identity
+
+F32 = mybir.dt.float32
+BF16 = mybir.dt.bfloat16
+I32 = mybir.dt.int32
+U32 = mybir.dt.uint32
+U8 = mybir.dt.uint8
+FP8X4 = mybir.dt.float8_e4m3fn_x4
+ALU = mybir.AluOpType
+ACT = mybir.ActivationFunctionType
+
+B, I, H = 256, 16384, 1024
+EPS = 1e-5
+FLOPS = 2 * B * (I + H) * H
+
+P = 128
+PACK = 4
+K_GROUP = P * PACK
+PAIRS = K_GROUP // 2
+B_TILES = B // P
+N_BANK = 512
+N_HALVES = H // N_BANK
+X_GROUPS = I // K_GROUP
+H_GROUPS = H // K_GROUP
+X_CHUNK = 4
+W_CHUNK = 2
+PLANES_PER_TILE = 4
+STREAM_BUFS = 11
+
+
+def load_weight_chunk(nc, stream, words, first_group):
+    chunk = stream.tile([P, W_CHUNK, PACK * H], U8, tag="chunk", align_bytes=64)
+    nc.sync.dma_start(
+        out=chunk[:].bitcast(I32),
+        in_=words[first_group : first_group + W_CHUNK].rearrange("g p n t -> p g (n t)").bitcast(I32),
+    )
+    return chunk
+
+
+def load_scale_planes(nc, planes, slot, scales, groups):
+    for quadrant in range(4):
+        first = 32 * quadrant
+        nc.sync.dma_start(
+            out=planes[first : first + 4 * len(groups), slot, :].bitcast(I32),
+            in_=scales[groups[0] : groups[-1] + 1, 4 * quadrant : 4 * quadrant + 4, :].bitcast(I32),
+        )
+
+
+def transpose_and_quantise(nc, psum, stage, identity, rows, n_groups, codes, planes):
+    words = rows.bitcast(F32)
+    grouped = stage.tile([P, X_CHUNK * B_TILES * P * PACK], BF16, tag="grouped", align_bytes=64)
+    grouped_words = grouped[:].bitcast(F32).rearrange("p (g t b u) -> p g t b u", g=X_CHUNK, t=B_TILES, u=2)
+    for g in range(n_groups):
+        bank = psum.tile([P, B_TILES, 2, P], F32, tag="bank")
+        for t in range(B_TILES):
+            for u in range(2):
+                nc.tensor.transpose(bank[:, t, u, :], words[:, t, PAIRS * g + u : PAIRS * (g + 1) : 2], identity[:])
+        side_by_side = bank[:].rearrange("p t u b -> p t b u")
+        if g % 4 == 0:
+            nc.vector.tensor_copy(out=grouped_words[:, g], in_=side_by_side)
+        else:
+            nc.scalar.copy(out=grouped_words[:, g], in_=side_by_side)
+    nc.vector.quantize_mx(
+        out=codes.bitcast(FP8X4),
+        scales=planes,
+        in_=grouped[:, : n_groups * B_TILES * P * PACK],
+    )
+
+
+def multiply_group(nc, acc, codes, planes, g, w_words, w_plane, start, stop):
+    for t in range(B_TILES):
+        for c in range(N_HALVES):
+            nc.tensor.matmul_mx(
+                out=acc[t][c][:],
+                lhsT=codes[:, g, t, :].bitcast(FP8X4),
+                lhsT_scale=planes[:, g, t, :],
+                rhs=w_words[:, PACK * N_BANK * c : PACK * N_BANK * (c + 1)].bitcast(FP8X4),
+                rhs_scale=w_plane[:, N_BANK * c : N_BANK * (c + 1)],
+                start=start,
+                stop=stop,
+            )
+
+
+def add_bias_and_measure(nc, work, small, acc_halves, bias, neg_half):
+    v = work.tile([P, H], F32, tag="v")
+    sums = small.tile([P, N_HALVES], F32, tag="sums")
+    for c in range(N_HALVES):
+        cols = slice(N_BANK * c, N_BANK * (c + 1))
+        nc.vector.scalar_tensor_tensor(
+            out=v[:, cols], in0=acc_halves[c][:], scalar=1.0, in1=bias[:, cols],
+            op0=ALU.mult, op1=ALU.add, accum_out=sums[:, c : c + 1],
+        )
+    neg_mean = small.tile([P, 1], F32, tag="neg_mean")
+    nc.vector.tensor_scalar(
+        out=neg_mean[:], in0=sums[:, 0:1], scalar1=sums[:, 1:2], scalar2=-1.0 / H, op0=ALU.add, op1=ALU.mult
+    )
+    squares = work.tile([P, H], BF16, tag="squares", bufs=2)
+    sum_sq = small.tile([P, 1], F32, tag="sum_sq")
+    nc.scalar.activation(out=squares[:], in_=v[:], func=ACT.Square, bias=neg_mean[:], scale=1.0, accum_out=sum_sq[:])
+    var_eps = small.tile([P, 1], F32, tag="var_eps")
+    nc.vector.tensor_scalar(out=var_eps[:], in0=sum_sq[:], scalar1=1.0 / H, scalar2=EPS, op0=ALU.mult, op1=ALU.add)
+    rstd = small.tile([P, 1], F32, tag="rstd")
+    nc.gpsimd.tensor_tensor(out=rstd[:], in0=var_eps[:], in1=neg_half[:], op=ALU.pow)
+    return v, neg_mean, rstd
+
+
+def tile_layernormgrucell_pb_k_kernel(
+    tc, x, h, r, z, W_in_words, W_in_scales, b_in, W_hn_words, W_hn_scales, b_hn, out
+):
+    nc = tc.nc
+    with ExitStack() as stack:
+        consts = stack.enter_context(tc.tile_pool(name="consts", bufs=1))
+        stream = stack.enter_context(tc.tile_pool(name="stream", bufs=STREAM_BUFS))
+        stage = stack.enter_context(tc.tile_pool(name="stage", bufs=2))
+        gates = stack.enter_context(tc.tile_pool(name="gates", bufs=1))
+        work = stack.enter_context(tc.tile_pool(name="work", bufs=2 * B_TILES))
+        small = stack.enter_context(tc.tile_pool(name="small", bufs=2 * B_TILES))
+        psum = stack.enter_context(tc.psum_pool(name="psum", bufs=8))
+
+        w_planes = consts.tile([P, X_GROUPS // PLANES_PER_TILE + 1, H], U8, align_bytes=64)
+        nc.vector.memset(w_planes[:].rearrange("p s n -> p (s n)").bitcast(I32), 0)
+        bias_rows = consts.tile([P, 2 * H], BF16)
+        nc.vector.memset(bias_rows[:].bitcast(I32), 0)
+        nc.scalar.dma_start(out=bias_rows[0:1, 0:H], in_=b_in.unsqueeze(0))
+        nc.scalar.dma_start(out=bias_rows[0:1, H : 2 * H], in_=b_hn.unsqueeze(0))
+        ones = consts.tile([P, P], BF16)
+        nc.vector.memset(ones[:], 1.0)
+        neg_half = consts.tile([P, 1], F32)
+        nc.gpsimd.memset(neg_half[:], -0.5)
+        identity = consts.tile([P, P], F32)
+        make_identity(nc, identity[:])
+        biases = consts.tile([P, 2 * H], BF16)
+        for j in range(2 * N_HALVES):
+            cols = slice(N_BANK * j, N_BANK * (j + 1))
+            spread = psum.tile([P, N_BANK], F32, tag="bank")
+            nc.tensor.matmul(out=spread[:], lhsT=ones[:], rhs=bias_rows[:, cols], start=True, stop=True)
+            nc.vector.tensor_copy(out=biases[:, cols], in_=spread[:])
+
+        x_codes = consts.tile([P, X_GROUPS, B_TILES, P], U32, align_bytes=64)
+        x_planes = consts.tile([P, X_GROUPS, B_TILES, P], U8, align_bytes=64)
+        x_rows = x.rearrange("(t p) k -> p t k", p=P)
+        for first in range(0, X_GROUPS, X_CHUNK):
+            x_chunk = stream.tile([P, B_TILES, X_CHUNK * K_GROUP], BF16, tag="chunk", align_bytes=64)
+            nc.sync.dma_start(out=x_chunk[:], in_=x_rows[:, :, K_GROUP * first : K_GROUP * (first + X_CHUNK)])
+            transpose_and_quantise(
+                nc, psum, stage, identity, x_chunk[:], X_CHUNK,
+                x_codes[:, first : first + X_CHUNK].rearrange("p g t b -> p (g t b)"),
+                x_planes[:, first : first + X_CHUNK].rearrange("p g t b -> p (g t b)"),
+            )
+        h_rows = gates.tile([P, B_TILES, H], BF16)
+        nc.sync.dma_start(out=h_rows[:], in_=h.rearrange("(t p) k -> p t k", p=P))
+        h_codes = consts.tile([P, H_GROUPS, B_TILES, P], U32, align_bytes=64)
+        h_planes = consts.tile([P, H_GROUPS, B_TILES, P], U8, align_bytes=64)
+        transpose_and_quantise(
+            nc, psum, stage, identity, h_rows[:], H_GROUPS,
+            h_codes[:].rearrange("p g t b -> p (g t b)"),
+            h_planes[:].rearrange("p g t b -> p (g t b)"),
+        )
+
+        w_hn = load_weight_chunk(nc, stream, W_hn_words, 0)
+        hn_slot = X_GROUPS // PLANES_PER_TILE
+        load_scale_planes(nc, w_planes, hn_slot, W_hn_scales, list(range(H_GROUPS)))
+        for slot in range(X_GROUPS // PLANES_PER_TILE):
+            first = PLANES_PER_TILE * slot
+            load_scale_planes(nc, w_planes, slot, W_in_scales, list(range(first, first + PLANES_PER_TILE)))
+
+        acc_h = [[psum.tile([P, N_BANK], F32, tag="bank", name="acc_h%d%d" % (t, c)) for c in range(N_HALVES)]
+                 for t in range(B_TILES)]
+        for g in range(H_GROUPS):
+            multiply_group(
+                nc, acc_h, h_codes, h_planes, g, w_hn[:, g, :], w_planes[4 * g : P, hn_slot, :],
+                start=(g == 0), stop=(g == H_GROUPS - 1),
+            )
+        h_n = []
+        for t in range(B_TILES):
+            v, neg_mean, rstd = add_bias_and_measure(nc, work, small, acc_h[t], biases[:, H : 2 * H], neg_half)
+            nc.vector.tensor_scalar(
+                out=v[:], in0=v[:], scalar1=neg_mean[:], scalar2=rstd[:], op0=ALU.add, op1=ALU.mult
+            )
+            h_n.append(v)
+
+        acc_i = [[psum.tile([P, N_BANK], F32, tag="bank", name="acc_i%d%d" % (t, c)) for c in range(N_HALVES)]
+                 for t in range(B_TILES)]
+
+        def multiply_chunks(first_group, end_group):
+            for first in range(first_group, end_group, W_CHUNK):
+                w_in = load_weight_chunk(nc, stream, W_in_words, first)
+                for g in range(first, first + W_CHUNK):
+                    multiply_group(
+                        nc, acc_i, x_codes, x_planes, g, w_in[:, g - first, :],
+                        w_planes[4 * (g % PLANES_PER_TILE) : P, g // PLANES_PER_TILE, :],
+                        start=(g == 0), stop=(g == X_GROUPS - 1),
+                    )
+
+        multiply_chunks(0, X_GROUPS // 2)
+        r_rows = gates.tile([P, B_TILES, H], BF16)
+        nc.sync.dma_start(out=r_rows[:], in_=r.rearrange("(t p) n -> p t n", p=P))
+        z_rows = gates.tile([P, B_TILES, H], BF16)
+        nc.sync.dma_start(out=z_rows[:], in_=z.rearrange("(t p) n -> p t n", p=P))
+        r_hn = gates.tile([P, B_TILES, H], F32)
+        one_minus_z = gates.tile([P, B_TILES, H], F32)
+        z_h = gates.tile([P, B_TILES, H], F32)
+        for t in range(B_TILES):
+            nc.vector.tensor_mul(out=r_hn[:, t, :], in0=r_rows[:, t, :], in1=h_n[t][:])
+            nc.vector.tensor_scalar(
+                out=one_minus_z[:, t, :], in0=z_rows[:, t, :], scalar1=-1.0, scalar2=1.0, op0=ALU.mult, op1=ALU.add
+            )
+            nc.vector.tensor_mul(out=z_h[:, t, :], in0=z_rows[:, t, :], in1=h_rows[:, t, :])
+        multiply_chunks(X_GROUPS // 2, X_GROUPS)
+
+        measured = [add_bias_and_measure(nc, work, small, acc_i[t], biases[:, 0:H], neg_half) for t in range(B_TILES)]
+        for t in range(B_TILES):
+            state, neg_mean, rstd = measured[t]
+            shift = small.tile([P, 1], F32, tag="shift")
+            nc.gpsimd.tensor_tensor(out=shift[:], in0=neg_mean[:], in1=rstd[:], op=ALU.mult)
+            halves = [slice(N_BANK * c, N_BANK * (c + 1)) for c in range(N_HALVES)]
+            for cols in halves:
+                nc.vector.scalar_tensor_tensor(
+                    out=state[:, cols], in0=state[:, cols], scalar=rstd[:], in1=r_hn[:, t, cols],
+                    op0=ALU.mult, op1=ALU.add,
+                )
+                nc.scalar.activation(out=state[:, cols], in_=state[:, cols], func=ACT.Tanh, bias=shift[:], scale=1.0)
+            for cols in halves:
+                nc.vector.tensor_mul(out=state[:, cols], in0=state[:, cols], in1=one_minus_z[:, t, cols])
+            for cols in halves:
+                nc.vector.tensor_add(out=state[:, cols], in0=state[:, cols], in1=z_h[:, t, cols])
+                nc.sync.dma_start(out=out[P * t : P * (t + 1), cols], in_=state[:, cols])

@@ -132,12 +132,6 @@ def tile_layernormgrucell_pb_k_kernel(
         nc.gpsimd.memset(neg_half[:], -0.5)
         identity = consts.tile([P, P], F32)
         make_identity(nc, identity[:])
-        biases = consts.tile([P, 2 * H], BF16)
-        for j in range(2 * N_HALVES):
-            cols = slice(N_BANK * j, N_BANK * (j + 1))
-            spread = psum.tile([P, N_BANK], F32, tag="bank")
-            nc.tensor.matmul(out=spread[:], lhsT=ones[:], rhs=bias_rows[:, cols], start=True, stop=True)
-            nc.vector.tensor_copy(out=biases[:, cols], in_=spread[:])
 
         x_codes = consts.tile([P, X_GROUPS, B_TILES, P], U32, align_bytes=64)
         x_planes = consts.tile([P, X_GROUPS, B_TILES, P], U8, align_bytes=64)
@@ -159,6 +153,13 @@ def tile_layernormgrucell_pb_k_kernel(
             h_codes[:].rearrange("p g t b -> p (g t b)"),
             h_planes[:].rearrange("p g t b -> p (g t b)"),
         )
+
+        biases = consts.tile([P, 2 * H], BF16)
+        for j in range(2 * N_HALVES):
+            cols = slice(N_BANK * j, N_BANK * (j + 1))
+            spread = psum.tile([P, N_BANK], F32, tag="bank")
+            nc.tensor.matmul(out=spread[:], lhsT=ones[:], rhs=bias_rows[:, cols], start=True, stop=True)
+            nc.vector.tensor_copy(out=biases[:, cols], in_=spread[:])
 
         w_hn = load_weight_chunk(nc, stream, W_hn_words, 0)
         hn_slot = X_GROUPS // PLANES_PER_TILE

@@ -27,7 +27,8 @@ X_GROUPS = I // K_GROUP
 H_GROUPS = H // K_GROUP
 X_CHUNK = 4
 W_CHUNK = 2
-PLANES_PER_TILE = 4
+PLANES_PER_SLOT = 4
+IN_SLOTS = X_GROUPS // PLANES_PER_SLOT
 STREAM_BUFS = 11
 
 
@@ -40,12 +41,14 @@ def load_weight_chunk(nc, stream, words, first_group):
     return chunk
 
 
-def load_scale_planes(nc, planes, slot, scales, groups):
-    for quadrant in range(4):
-        first = 32 * quadrant
-        nc.sync.dma_start(
-            out=planes[first : first + 4 * len(groups), slot, :].bitcast(I32),
-            in_=scales[groups[0] : groups[-1] + 1, 4 * quadrant : 4 * quadrant + 4, :].bitcast(I32),
+def load_scale_planes(nc, planes, scales):
+    per_slot = scales.shape[0] // planes.shape[1]
+    by_row = scales.rearrange("(s j) q n -> q j s n", j=per_slot)
+    for q in range(scales.shape[1]):
+        first = 32 * (q // 4) + q % 4
+        nc.gpsimd.dma_start(
+            out=planes[first : first + 4 * per_slot : 4, :, :].bitcast(F32),
+            in_=by_row[q].bitcast(F32),
         )
 
 
@@ -120,7 +123,7 @@ def tile_layernormgrucell_pb_k_kernel(
         small = stack.enter_context(tc.tile_pool(name="small", bufs=2 * B_TILES))
         psum = stack.enter_context(tc.psum_pool(name="psum", bufs=8))
 
-        w_planes = consts.tile([P, X_GROUPS // PLANES_PER_TILE + 1, H], U8, align_bytes=64)
+        w_planes = consts.tile([P, IN_SLOTS + 1, H], U8, align_bytes=64)
         nc.vector.memset(w_planes[:].rearrange("p s n -> p (s n)").bitcast(I32), 0)
         bias_rows = consts.tile([P, 2 * H], BF16)
         nc.vector.memset(bias_rows[:].bitcast(I32), 0)
@@ -132,6 +135,8 @@ def tile_layernormgrucell_pb_k_kernel(
         nc.gpsimd.memset(neg_half[:], -0.5)
         identity = consts.tile([P, P], F32)
         make_identity(nc, identity[:])
+        load_scale_planes(nc, w_planes[:, 0:IN_SLOTS, :], W_in_scales)
+        load_scale_planes(nc, w_planes[:, IN_SLOTS : IN_SLOTS + 1, :], W_hn_scales)
 
         x_codes = consts.tile([P, X_GROUPS, B_TILES, P], U32, align_bytes=64)
         x_planes = consts.tile([P, X_GROUPS, B_TILES, P], U8, align_bytes=64)
@@ -161,28 +166,6 @@ def tile_layernormgrucell_pb_k_kernel(
             nc.tensor.matmul(out=spread[:], lhsT=ones[:], rhs=bias_rows[:, cols], start=True, stop=True)
             nc.vector.tensor_copy(out=biases[:, cols], in_=spread[:])
 
-        w_hn = load_weight_chunk(nc, stream, W_hn_words, 0)
-        hn_slot = X_GROUPS // PLANES_PER_TILE
-        load_scale_planes(nc, w_planes, hn_slot, W_hn_scales, list(range(H_GROUPS)))
-        for slot in range(X_GROUPS // PLANES_PER_TILE):
-            first = PLANES_PER_TILE * slot
-            load_scale_planes(nc, w_planes, slot, W_in_scales, list(range(first, first + PLANES_PER_TILE)))
-
-        acc_h = [[psum.tile([P, N_BANK], F32, tag="bank", name="acc_h%d%d" % (t, c)) for c in range(N_HALVES)]
-                 for t in range(B_TILES)]
-        for g in range(H_GROUPS):
-            multiply_group(
-                nc, acc_h, h_codes, h_planes, g, w_hn[:, g, :], w_planes[4 * g : P, hn_slot, :],
-                start=(g == 0), stop=(g == H_GROUPS - 1),
-            )
-        h_n = []
-        for t in range(B_TILES):
-            v, neg_mean, rstd = add_bias_and_measure(nc, work, small, acc_h[t], biases[:, H : 2 * H], neg_half)
-            nc.vector.tensor_scalar(
-                out=v[:], in0=v[:], scalar1=neg_mean[:], scalar2=rstd[:], op0=ALU.add, op1=ALU.mult
-            )
-            h_n.append(v)
-
         acc_i = [[psum.tile([P, N_BANK], F32, tag="bank", name="acc_i%d%d" % (t, c)) for c in range(N_HALVES)]
                  for t in range(B_TILES)]
 
@@ -192,11 +175,20 @@ def tile_layernormgrucell_pb_k_kernel(
                 for g in range(first, first + W_CHUNK):
                     multiply_group(
                         nc, acc_i, x_codes, x_planes, g, w_in[:, g - first, :],
-                        w_planes[4 * (g % PLANES_PER_TILE) : P, g // PLANES_PER_TILE, :],
+                        w_planes[4 * (g % PLANES_PER_SLOT) : P, g // PLANES_PER_SLOT, :],
                         start=(g == 0), stop=(g == X_GROUPS - 1),
                     )
 
         multiply_chunks(0, X_GROUPS // 2)
+
+        w_hn = load_weight_chunk(nc, stream, W_hn_words, 0)
+        acc_h = [[psum.tile([P, N_BANK], F32, tag="bank", name="acc_h%d%d" % (t, c)) for c in range(N_HALVES)]
+                 for t in range(B_TILES)]
+        for g in range(H_GROUPS):
+            multiply_group(
+                nc, acc_h, h_codes, h_planes, g, w_hn[:, g, :], w_planes[4 * g : P, IN_SLOTS, :],
+                start=(g == 0), stop=(g == H_GROUPS - 1),
+            )
         r_rows = gates.tile([P, B_TILES, H], BF16)
         nc.sync.dma_start(out=r_rows[:], in_=r.rearrange("(t p) n -> p t n", p=P))
         z_rows = gates.tile([P, B_TILES, H], BF16)
@@ -205,11 +197,16 @@ def tile_layernormgrucell_pb_k_kernel(
         one_minus_z = gates.tile([P, B_TILES, H], F32)
         z_h = gates.tile([P, B_TILES, H], F32)
         for t in range(B_TILES):
-            nc.vector.tensor_mul(out=r_hn[:, t, :], in0=r_rows[:, t, :], in1=h_n[t][:])
+            v, neg_mean, rstd = add_bias_and_measure(nc, work, small, acc_h[t], biases[:, H : 2 * H], neg_half)
+            nc.vector.tensor_scalar(
+                out=v[:], in0=v[:], scalar1=neg_mean[:], scalar2=rstd[:], op0=ALU.add, op1=ALU.mult
+            )
+            nc.vector.tensor_mul(out=r_hn[:, t, :], in0=r_rows[:, t, :], in1=v[:])
             nc.vector.tensor_scalar(
                 out=one_minus_z[:, t, :], in0=z_rows[:, t, :], scalar1=-1.0, scalar2=1.0, op0=ALU.mult, op1=ALU.add
             )
             nc.vector.tensor_mul(out=z_h[:, t, :], in0=z_rows[:, t, :], in1=h_rows[:, t, :])
+
         multiply_chunks(X_GROUPS // 2, X_GROUPS)
 
         measured = [add_bias_and_measure(nc, work, small, acc_i[t], biases[:, 0:H], neg_half) for t in range(B_TILES)]

@@ -42,14 +42,22 @@ def load_weight_chunk(nc, stream, words, first_group):
 
 
 def load_scale_planes(nc, planes, scales):
-    per_slot = scales.shape[0] // planes.shape[1]
+    n_slots = planes.shape[1]
+    per_slot = scales.shape[0] // n_slots
     by_row = scales.rearrange("(s j) q n -> q j s n", j=per_slot)
-    for q in range(scales.shape[1]):
-        first = 32 * (q // 4) + q % 4
-        nc.gpsimd.dma_start(
-            out=planes[first : first + 4 * per_slot : 4, :, :].bitcast(F32),
-            in_=by_row[q].bitcast(F32),
-        )
+    for quadrant in range(4):
+        first = 32 * quadrant
+        if n_slots == 1:
+            nc.sync.dma_start(
+                out=planes[first : first + 4 * per_slot, 0, :].bitcast(I32),
+                in_=scales[:, 4 * quadrant : 4 * quadrant + 4, :].bitcast(I32),
+            )
+        else:
+            for row in range(4):
+                nc.sync.dma_start(
+                    out=planes[first + row : first + row + 4 * per_slot : 4, :, :].bitcast(I32),
+                    in_=by_row[4 * quadrant + row].bitcast(I32),
+                )
 
 
 def transpose_and_quantise(nc, psum, stage, identity, rows, n_groups, codes, planes):
@@ -135,8 +143,6 @@ def tile_layernormgrucell_pb_k_kernel(
         nc.gpsimd.memset(neg_half[:], -0.5)
         identity = consts.tile([P, P], F32)
         make_identity(nc, identity[:])
-        load_scale_planes(nc, w_planes[:, 0:IN_SLOTS, :], W_in_scales)
-        load_scale_planes(nc, w_planes[:, IN_SLOTS : IN_SLOTS + 1, :], W_hn_scales)
 
         x_codes = consts.tile([P, X_GROUPS, B_TILES, P], U32, align_bytes=64)
         x_planes = consts.tile([P, X_GROUPS, B_TILES, P], U8, align_bytes=64)
@@ -166,6 +172,25 @@ def tile_layernormgrucell_pb_k_kernel(
             nc.tensor.matmul(out=spread[:], lhsT=ones[:], rhs=bias_rows[:, cols], start=True, stop=True)
             nc.vector.tensor_copy(out=biases[:, cols], in_=spread[:])
 
+        w_hn = load_weight_chunk(nc, stream, W_hn_words, 0)
+        load_scale_planes(nc, w_planes[:, IN_SLOTS : IN_SLOTS + 1, :], W_hn_scales)
+        load_scale_planes(nc, w_planes[:, 0:IN_SLOTS, :], W_in_scales)
+
+        acc_h = [[psum.tile([P, N_BANK], F32, tag="bank", name="acc_h%d%d" % (t, c)) for c in range(N_HALVES)]
+                 for t in range(B_TILES)]
+        for g in range(H_GROUPS):
+            multiply_group(
+                nc, acc_h, h_codes, h_planes, g, w_hn[:, g, :], w_planes[4 * g : P, IN_SLOTS, :],
+                start=(g == 0), stop=(g == H_GROUPS - 1),
+            )
+        h_n = []
+        for t in range(B_TILES):
+            v, neg_mean, rstd = add_bias_and_measure(nc, work, small, acc_h[t], biases[:, H : 2 * H], neg_half)
+            nc.vector.tensor_scalar(
+                out=v[:], in0=v[:], scalar1=neg_mean[:], scalar2=rstd[:], op0=ALU.add, op1=ALU.mult
+            )
+            h_n.append(v)
+
         acc_i = [[psum.tile([P, N_BANK], F32, tag="bank", name="acc_i%d%d" % (t, c)) for c in range(N_HALVES)]
                  for t in range(B_TILES)]
 
@@ -180,15 +205,6 @@ def tile_layernormgrucell_pb_k_kernel(
                     )
 
         multiply_chunks(0, X_GROUPS // 2)
-
-        w_hn = load_weight_chunk(nc, stream, W_hn_words, 0)
-        acc_h = [[psum.tile([P, N_BANK], F32, tag="bank", name="acc_h%d%d" % (t, c)) for c in range(N_HALVES)]
-                 for t in range(B_TILES)]
-        for g in range(H_GROUPS):
-            multiply_group(
-                nc, acc_h, h_codes, h_planes, g, w_hn[:, g, :], w_planes[4 * g : P, IN_SLOTS, :],
-                start=(g == 0), stop=(g == H_GROUPS - 1),
-            )
         r_rows = gates.tile([P, B_TILES, H], BF16)
         nc.sync.dma_start(out=r_rows[:], in_=r.rearrange("(t p) n -> p t n", p=P))
         z_rows = gates.tile([P, B_TILES, H], BF16)
@@ -197,16 +213,11 @@ def tile_layernormgrucell_pb_k_kernel(
         one_minus_z = gates.tile([P, B_TILES, H], F32)
         z_h = gates.tile([P, B_TILES, H], F32)
         for t in range(B_TILES):
-            v, neg_mean, rstd = add_bias_and_measure(nc, work, small, acc_h[t], biases[:, H : 2 * H], neg_half)
-            nc.vector.tensor_scalar(
-                out=v[:], in0=v[:], scalar1=neg_mean[:], scalar2=rstd[:], op0=ALU.add, op1=ALU.mult
-            )
-            nc.vector.tensor_mul(out=r_hn[:, t, :], in0=r_rows[:, t, :], in1=v[:])
+            nc.vector.tensor_mul(out=r_hn[:, t, :], in0=r_rows[:, t, :], in1=h_n[t][:])
             nc.vector.tensor_scalar(
                 out=one_minus_z[:, t, :], in0=z_rows[:, t, :], scalar1=-1.0, scalar2=1.0, op0=ALU.mult, op1=ALU.add
             )
             nc.vector.tensor_mul(out=z_h[:, t, :], in0=z_rows[:, t, :], in1=h_rows[:, t, :])
-
         multiply_chunks(X_GROUPS // 2, X_GROUPS)
 
         measured = [add_bias_and_measure(nc, work, small, acc_i[t], biases[:, 0:H], neg_half) for t in range(B_TILES)]

@@ -29,7 +29,8 @@ X_CHUNK = 4
 W_CHUNK = 2
 PLANES_PER_SLOT = 4
 IN_SLOTS = X_GROUPS // PLANES_PER_SLOT
-STREAM_BUFS = 11
+X_BUFS = 3
+W_BUFS = 11
 
 
 def load_weight_chunk(nc, stream, words, first_group):
@@ -124,101 +125,113 @@ def tile_layernormgrucell_pb_k_kernel(
     nc = tc.nc
     with ExitStack() as stack:
         consts = stack.enter_context(tc.tile_pool(name="consts", bufs=1))
-        stream = stack.enter_context(tc.tile_pool(name="stream", bufs=STREAM_BUFS))
+        x_stream = stack.enter_context(tc.tile_pool(name="x_stream", bufs=X_BUFS))
+        w_stream = stack.enter_context(tc.tile_pool(name="w_stream", bufs=W_BUFS))
         stage = stack.enter_context(tc.tile_pool(name="stage", bufs=2))
+        quantised = stack.enter_context(tc.tile_pool(name="quantised", bufs=3))
         gates = stack.enter_context(tc.tile_pool(name="gates", bufs=1))
         work = stack.enter_context(tc.tile_pool(name="work", bufs=2 * B_TILES))
         small = stack.enter_context(tc.tile_pool(name="small", bufs=2 * B_TILES))
-        psum = stack.enter_context(tc.psum_pool(name="psum", bufs=8))
+        psum = stack.enter_context(tc.psum_pool(name="psum", bufs=4))
+        sums_psum = stack.enter_context(tc.psum_pool(name="sums_psum", bufs=1))
 
-        w_planes = consts.tile([P, IN_SLOTS + 1, H], U8, align_bytes=64)
-        nc.vector.memset(w_planes[:].rearrange("p s n -> p (s n)").bitcast(I32), 0)
+        identity = consts.tile([P, P], F32)
+        make_identity(nc, identity[:])
         bias_rows = consts.tile([P, 2 * H], BF16)
         nc.vector.memset(bias_rows[:].bitcast(I32), 0)
-        nc.scalar.dma_start(out=bias_rows[0:1, 0:H], in_=b_in.unsqueeze(0))
-        nc.scalar.dma_start(out=bias_rows[0:1, H : 2 * H], in_=b_hn.unsqueeze(0))
+        w_planes = consts.tile([P, IN_SLOTS + 1, H], U8, align_bytes=64)
+        nc.vector.memset(w_planes[:].rearrange("p s n -> p (s n)").bitcast(I32), 0)
         ones = consts.tile([P, P], BF16)
         nc.vector.memset(ones[:], 1.0)
         neg_half = consts.tile([P, 1], F32)
         nc.gpsimd.memset(neg_half[:], -0.5)
-        identity = consts.tile([P, P], F32)
-        make_identity(nc, identity[:])
 
-        x_codes = consts.tile([P, X_GROUPS, B_TILES, P], U32, align_bytes=64)
-        x_planes = consts.tile([P, X_GROUPS, B_TILES, P], U8, align_bytes=64)
         x_rows = x.rearrange("(t p) k -> p t k", p=P)
-        for first in range(0, X_GROUPS, X_CHUNK):
-            x_chunk = stream.tile([P, B_TILES, X_CHUNK * K_GROUP], BF16, tag="chunk", align_bytes=64)
+
+        def load_x(first):
+            x_chunk = x_stream.tile([P, B_TILES, X_CHUNK * K_GROUP], BF16, tag="chunk", align_bytes=64)
             nc.sync.dma_start(out=x_chunk[:], in_=x_rows[:, :, K_GROUP * first : K_GROUP * (first + X_CHUNK)])
+            return x_chunk
+
+        def quantise_rows(rows, n_groups):
+            codes = quantised.tile([P, X_CHUNK, B_TILES, P], U32, tag="codes", align_bytes=64)
+            planes = quantised.tile([P, X_CHUNK, B_TILES, P], U8, tag="planes", align_bytes=64)
             transpose_and_quantise(
-                nc, psum, stage, identity, x_chunk[:], X_CHUNK,
-                x_codes[:, first : first + X_CHUNK].rearrange("p g t b -> p (g t b)"),
-                x_planes[:, first : first + X_CHUNK].rearrange("p g t b -> p (g t b)"),
+                nc, psum, stage, identity, rows, n_groups,
+                codes[:, :n_groups].rearrange("p g t b -> p (g t b)"),
+                planes[:, :n_groups].rearrange("p g t b -> p (g t b)"),
             )
-        h_rows = gates.tile([P, B_TILES, H], BF16)
-        nc.sync.dma_start(out=h_rows[:], in_=h.rearrange("(t p) k -> p t k", p=P))
-        h_codes = consts.tile([P, H_GROUPS, B_TILES, P], U32, align_bytes=64)
-        h_planes = consts.tile([P, H_GROUPS, B_TILES, P], U8, align_bytes=64)
-        transpose_and_quantise(
-            nc, psum, stage, identity, h_rows[:], H_GROUPS,
-            h_codes[:].rearrange("p g t b -> p (g t b)"),
-            h_planes[:].rearrange("p g t b -> p (g t b)"),
-        )
+            return codes, planes
 
-        biases = consts.tile([P, 2 * H], BF16)
-        for j in range(2 * N_HALVES):
-            cols = slice(N_BANK * j, N_BANK * (j + 1))
-            spread = psum.tile([P, N_BANK], F32, tag="bank")
-            nc.tensor.matmul(out=spread[:], lhsT=ones[:], rhs=bias_rows[:, cols], start=True, stop=True)
-            nc.vector.tensor_copy(out=biases[:, cols], in_=spread[:])
+        def open_sums(kind):
+            return [[sums_psum.tile([P, N_BANK], F32, tag="sums%d%d" % (t, c), name="%s%d%d" % (kind, t, c))
+                     for c in range(N_HALVES)] for t in range(B_TILES)]
 
-        w_hn = load_weight_chunk(nc, stream, W_hn_words, 0)
-        load_scale_planes(nc, w_planes[:, IN_SLOTS : IN_SLOTS + 1, :], W_hn_scales)
-        load_scale_planes(nc, w_planes[:, 0:IN_SLOTS, :], W_in_scales)
+        with tc.manual_schedule(engines={mybir.EngineType.PE, mybir.EngineType.SP}):
+            h_rows = gates.tile([P, B_TILES, H], BF16)
+            nc.sync.dma_start(out=h_rows[:], in_=h.rearrange("(t p) k -> p t k", p=P))
+            x_chunk = load_x(0)
+            nc.sync.dma_start(out=bias_rows[0:1, 0:H], in_=b_in.unsqueeze(0))
+            nc.sync.dma_start(out=bias_rows[0:1, H : 2 * H], in_=b_hn.unsqueeze(0))
+            h_codes, h_planes = quantise_rows(h_rows[:], H_GROUPS)
 
-        acc_h = [[psum.tile([P, N_BANK], F32, tag="bank", name="acc_h%d%d" % (t, c)) for c in range(N_HALVES)]
-                 for t in range(B_TILES)]
-        for g in range(H_GROUPS):
-            multiply_group(
-                nc, acc_h, h_codes, h_planes, g, w_hn[:, g, :], w_planes[4 * g : P, IN_SLOTS, :],
-                start=(g == 0), stop=(g == H_GROUPS - 1),
-            )
-        h_n = []
-        for t in range(B_TILES):
-            v, neg_mean, rstd = add_bias_and_measure(nc, work, small, acc_h[t], biases[:, H : 2 * H], neg_half)
-            nc.vector.tensor_scalar(
-                out=v[:], in0=v[:], scalar1=neg_mean[:], scalar2=rstd[:], op0=ALU.add, op1=ALU.mult
-            )
-            h_n.append(v)
+            w_hn = load_weight_chunk(nc, w_stream, W_hn_words, 0)
+            load_scale_planes(nc, w_planes[:, IN_SLOTS : IN_SLOTS + 1, :], W_hn_scales)
+            load_scale_planes(nc, w_planes[:, 0:IN_SLOTS, :], W_in_scales)
+            codes, planes = quantise_rows(x_chunk[:], X_CHUNK)
 
-        acc_i = [[psum.tile([P, N_BANK], F32, tag="bank", name="acc_i%d%d" % (t, c)) for c in range(N_HALVES)]
-                 for t in range(B_TILES)]
+            biases = consts.tile([P, 2 * H], BF16)
+            for j in range(2 * N_HALVES):
+                cols = slice(N_BANK * j, N_BANK * (j + 1))
+                spread = psum.tile([P, N_BANK], F32, tag="bank")
+                nc.tensor.matmul(out=spread[:], lhsT=ones[:], rhs=bias_rows[:, cols], start=True, stop=True)
+                nc.vector.tensor_copy(out=biases[:, cols], in_=spread[:])
 
-        def multiply_chunks(first_group, end_group):
-            for first in range(first_group, end_group, W_CHUNK):
-                w_in = load_weight_chunk(nc, stream, W_in_words, first)
-                for g in range(first, first + W_CHUNK):
+            acc_h = open_sums("acc_h")
+            for g in range(H_GROUPS):
+                multiply_group(
+                    nc, acc_h, h_codes, h_planes, g, w_hn[:, g, :], w_planes[4 * g : P, IN_SLOTS, :],
+                    start=(g == 0), stop=(g == H_GROUPS - 1),
+                )
+            h_n = []
+            for t in range(B_TILES):
+                v, neg_mean, rstd = add_bias_and_measure(nc, work, small, acc_h[t], biases[:, H : 2 * H], neg_half)
+                nc.vector.tensor_scalar(
+                    out=v[:], in0=v[:], scalar1=neg_mean[:], scalar2=rstd[:], op0=ALU.add, op1=ALU.mult
+                )
+                h_n.append(v)
+
+            acc_i = open_sums("acc_i")
+            for first in range(0, X_GROUPS, X_CHUNK):
+                last_chunk = first + X_CHUNK == X_GROUPS
+                if not last_chunk:
+                    x_chunk = load_x(first + X_CHUNK)
+                w_in = [load_weight_chunk(nc, w_stream, W_in_words, g) for g in range(first, first + X_CHUNK, W_CHUNK)]
+                if first == X_GROUPS // 2:
+                    r_rows = gates.tile([P, B_TILES, H], BF16)
+                    nc.sync.dma_start(out=r_rows[:], in_=r.rearrange("(t p) n -> p t n", p=P))
+                    z_rows = gates.tile([P, B_TILES, H], BF16)
+                    nc.sync.dma_start(out=z_rows[:], in_=z.rearrange("(t p) n -> p t n", p=P))
+                if not last_chunk:
+                    next_codes, next_planes = quantise_rows(x_chunk[:], X_CHUNK)
+                for g in range(first, first + X_CHUNK):
                     multiply_group(
-                        nc, acc_i, x_codes, x_planes, g, w_in[:, g - first, :],
+                        nc, acc_i, codes, planes, g - first, w_in[(g - first) // W_CHUNK][:, g % W_CHUNK, :],
                         w_planes[4 * (g % PLANES_PER_SLOT) : P, g // PLANES_PER_SLOT, :],
                         start=(g == 0), stop=(g == X_GROUPS - 1),
                     )
-
-        multiply_chunks(0, X_GROUPS // 2)
-        r_rows = gates.tile([P, B_TILES, H], BF16)
-        nc.sync.dma_start(out=r_rows[:], in_=r.rearrange("(t p) n -> p t n", p=P))
-        z_rows = gates.tile([P, B_TILES, H], BF16)
-        nc.sync.dma_start(out=z_rows[:], in_=z.rearrange("(t p) n -> p t n", p=P))
-        r_hn = gates.tile([P, B_TILES, H], F32)
-        one_minus_z = gates.tile([P, B_TILES, H], F32)
-        z_h = gates.tile([P, B_TILES, H], F32)
-        for t in range(B_TILES):
-            nc.vector.tensor_mul(out=r_hn[:, t, :], in0=r_rows[:, t, :], in1=h_n[t][:])
-            nc.vector.tensor_scalar(
-                out=one_minus_z[:, t, :], in0=z_rows[:, t, :], scalar1=-1.0, scalar2=1.0, op0=ALU.mult, op1=ALU.add
-            )
-            nc.vector.tensor_mul(out=z_h[:, t, :], in0=z_rows[:, t, :], in1=h_rows[:, t, :])
-        multiply_chunks(X_GROUPS // 2, X_GROUPS)
+                codes, planes = next_codes, next_planes
+                if first == X_GROUPS // 2:
+                    r_hn = gates.tile([P, B_TILES, H], F32)
+                    one_minus_z = gates.tile([P, B_TILES, H], F32)
+                    z_h = gates.tile([P, B_TILES, H], F32)
+                    for t in range(B_TILES):
+                        nc.vector.tensor_mul(out=r_hn[:, t, :], in0=r_rows[:, t, :], in1=h_n[t][:])
+                        nc.vector.tensor_scalar(
+                            out=one_minus_z[:, t, :], in0=z_rows[:, t, :], scalar1=-1.0, scalar2=1.0,
+                            op0=ALU.mult, op1=ALU.add,
+                        )
+                        nc.vector.tensor_mul(out=z_h[:, t, :], in0=z_rows[:, t, :], in1=h_rows[:, t, :])
 
         measured = [add_bias_and_measure(nc, work, small, acc_i[t], biases[:, 0:H], neg_half) for t in range(B_TILES)]
         for t in range(B_TILES):

@@ -82,41 +82,86 @@ def transpose_and_quantise(nc, psum, stage, identity, rows, n_groups, codes, pla
     )
 
 
+def multiply(nc, acc_half, codes, planes, g, t, w_words, w_plane, start, stop):
+    nc.tensor.matmul_mx(
+        out=acc_half[:],
+        lhsT=codes[:, g, t, :].bitcast(FP8X4),
+        lhsT_scale=planes[:, g, t, :],
+        rhs=w_words.bitcast(FP8X4),
+        rhs_scale=w_plane,
+        start=start,
+        stop=stop,
+    )
+
+
 def multiply_group(nc, acc, codes, planes, g, w_words, w_plane, start, stop):
     for t in range(B_TILES):
         for c in range(N_HALVES):
-            nc.tensor.matmul_mx(
-                out=acc[t][c][:],
-                lhsT=codes[:, g, t, :].bitcast(FP8X4),
-                lhsT_scale=planes[:, g, t, :],
-                rhs=w_words[:, PACK * N_BANK * c : PACK * N_BANK * (c + 1)].bitcast(FP8X4),
-                rhs_scale=w_plane[:, N_BANK * c : N_BANK * (c + 1)],
-                start=start,
-                stop=stop,
+            multiply(
+                nc, acc[t][c], codes, planes, g, t, w_words[:, PACK * N_BANK * c : PACK * N_BANK * (c + 1)],
+                w_plane[:, N_BANK * c : N_BANK * (c + 1)], start, stop,
             )
 
 
-def add_bias_and_measure(nc, work, small, acc_halves, bias, neg_half):
-    v = work.tile([P, H], F32, tag="v")
-    sums = small.tile([P, N_HALVES], F32, tag="sums")
-    for c in range(N_HALVES):
-        cols = slice(N_BANK * c, N_BANK * (c + 1))
-        nc.vector.scalar_tensor_tensor(
-            out=v[:, cols], in0=acc_halves[c][:], scalar=1.0, in1=bias[:, cols],
-            op0=ALU.mult, op1=ALU.add, accum_out=sums[:, c : c + 1],
-        )
-    neg_mean = small.tile([P, 1], F32, tag="neg_mean")
-    nc.vector.tensor_scalar(
-        out=neg_mean[:], in0=sums[:, 0:1], scalar1=sums[:, 1:2], scalar2=-1.0 / H, op0=ALU.add, op1=ALU.mult
+def new_norm(work, small, label):
+    return {
+        "v": work.tile([P, H], F32, tag="v", name="v_" + label),
+        "sums": small.tile([P, N_HALVES], F32, tag="sums", name="sums_" + label),
+        "neg_half_mean": small.tile([P, 1], F32, tag="neg_half_mean", name="neg_half_mean_" + label),
+        "centre": small.tile([P, 1], F32, tag="centre", name="centre_" + label),
+        "gap_sq": small.tile([P, 1], F32, tag="gap_sq", name="gap_sq_" + label),
+        "sum_sq": small.tile([P, N_HALVES], F32, tag="sum_sq", name="sum_sq_" + label),
+        "neg_mean": small.tile([P, 1], F32, tag="neg_mean", name="neg_mean_" + label),
+        "mean_sq": small.tile([P, 1], F32, tag="mean_sq", name="mean_sq_" + label),
+        "var_eps": small.tile([P, 1], F32, tag="var_eps", name="var_eps_" + label),
+        "rstd": small.tile([P, 1], F32, tag="rstd", name="rstd_" + label),
+        "shift": small.tile([P, 1], F32, tag="shift", name="shift_" + label),
+    }
+
+
+def add_bias(nc, norm, c, acc_half, bias):
+    cols = slice(N_BANK * c, N_BANK * (c + 1))
+    nc.vector.scalar_tensor_tensor(
+        out=norm["v"][:, cols], in0=acc_half[:], scalar=1.0, in1=bias[:, cols],
+        op0=ALU.mult, op1=ALU.add, accum_out=norm["sums"][:, c : c + 1],
     )
-    squares = work.tile([P, H], BF16, tag="squares", bufs=2)
-    sum_sq = small.tile([P, 1], F32, tag="sum_sq")
-    nc.scalar.activation(out=squares[:], in_=v[:], func=ACT.Square, bias=neg_mean[:], scale=1.0, accum_out=sum_sq[:])
-    var_eps = small.tile([P, 1], F32, tag="var_eps")
-    nc.vector.tensor_scalar(out=var_eps[:], in0=sum_sq[:], scalar1=1.0 / H, scalar2=EPS, op0=ALU.mult, op1=ALU.add)
-    rstd = small.tile([P, 1], F32, tag="rstd")
-    nc.gpsimd.tensor_tensor(out=rstd[:], in0=var_eps[:], in1=neg_half[:], op=ALU.pow)
-    return v, neg_mean, rstd
+
+
+def square_half(nc, work, norm, c):
+    cols = slice(N_BANK * c, N_BANK * (c + 1))
+    total = norm["sums"][:, c : c + 1]
+    if c == 0:
+        nc.scalar.activation(out=norm["centre"][:], in_=total, func=ACT.Copy, scale=-2.0 / H)
+        nc.scalar.activation(out=norm["neg_half_mean"][:], in_=total, func=ACT.Copy, scale=-1.0 / H)
+    else:
+        nc.scalar.activation(
+            out=norm["gap_sq"][:], in_=total, func=ACT.Square, bias=norm["neg_half_mean"][:], scale=1.0 / H
+        )
+    squares = work.tile([P, N_BANK], BF16, tag="squares", bufs=2)
+    nc.scalar.activation(
+        out=squares[:], in_=norm["v"][:, cols], func=ACT.Square, bias=norm["centre"][:], scale=1.0,
+        accum_out=norm["sum_sq"][:, c : c + 1],
+    )
+    if c == 1:
+        nc.scalar.activation(
+            out=norm["neg_mean"][:], in_=total, func=ACT.Identity, bias=norm["neg_half_mean"][:], scale=-1.0 / H
+        )
+
+
+def finish_norm(nc, norm, neg_half):
+    nc.vector.tensor_scalar(
+        out=norm["mean_sq"][:], in0=norm["sum_sq"][:, 0:1], scalar1=norm["sum_sq"][:, 1:2], scalar2=1.0 / H,
+        op0=ALU.add, op1=ALU.mult,
+    )
+    nc.vector.tensor_scalar(
+        out=norm["var_eps"][:], in0=norm["mean_sq"][:], scalar1=norm["gap_sq"][:], scalar2=EPS,
+        op0=ALU.subtract, op1=ALU.add,
+    )
+    nc.gpsimd.tensor_tensor(out=norm["rstd"][:], in0=norm["var_eps"][:], in1=neg_half[:], op=ALU.pow)
+
+
+def make_shift(nc, norm):
+    nc.scalar.activation(out=norm["shift"][:], in_=norm["neg_mean"][:], func=ACT.Copy, scale=norm["rstd"][:])
 
 
 def tile_layernormgrucell_pb_k_kernel(
@@ -167,7 +212,7 @@ def tile_layernormgrucell_pb_k_kernel(
             return [[sums_psum.tile([P, N_BANK], F32, tag="sums%d%d" % (t, c), name="%s%d%d" % (kind, t, c))
                      for c in range(N_HALVES)] for t in range(B_TILES)]
 
-        with tc.manual_schedule(engines={mybir.EngineType.PE, mybir.EngineType.SP}):
+        with tc.manual_schedule():
             h_rows = gates.tile([P, B_TILES, H], BF16)
             nc.sync.dma_start(out=h_rows[:], in_=h.rearrange("(t p) k -> p t k", p=P))
             x_chunk = load_x(0)
@@ -193,60 +238,105 @@ def tile_layernormgrucell_pb_k_kernel(
                     nc, acc_h, h_codes, h_planes, g, w_hn[:, g, :], w_planes[4 * g : P, IN_SLOTS, :],
                     start=(g == 0), stop=(g == H_GROUPS - 1),
                 )
-            h_n = []
+            norms_h = [new_norm(work, small, "h%d" % t) for t in range(B_TILES)]
             for t in range(B_TILES):
-                v, neg_mean, rstd = add_bias_and_measure(nc, work, small, acc_h[t], biases[:, H : 2 * H], neg_half)
-                nc.vector.tensor_scalar(
-                    out=v[:], in0=v[:], scalar1=neg_mean[:], scalar2=rstd[:], op0=ALU.add, op1=ALU.mult
-                )
-                h_n.append(v)
+                for c in range(N_HALVES):
+                    add_bias(nc, norms_h[t], c, acc_h[t][c], biases[:, H : 2 * H])
 
             acc_i = open_sums("acc_i")
+            norms = [new_norm(work, small, "i%d" % t) for t in range(B_TILES)]
             for first in range(0, X_GROUPS, X_CHUNK):
-                last_chunk = first + X_CHUNK == X_GROUPS
-                if not last_chunk:
+                groups = range(first, first + X_CHUNK)
+                w_plane = {g: w_planes[4 * (g % PLANES_PER_SLOT) : P, g // PLANES_PER_SLOT, :] for g in groups}
+                if first + X_CHUNK < X_GROUPS:
                     x_chunk = load_x(first + X_CHUNK)
-                w_in = [load_weight_chunk(nc, w_stream, W_in_words, g) for g in range(first, first + X_CHUNK, W_CHUNK)]
-                if first == X_GROUPS // 2:
-                    r_rows = gates.tile([P, B_TILES, H], BF16)
-                    nc.sync.dma_start(out=r_rows[:], in_=r.rearrange("(t p) n -> p t n", p=P))
-                    z_rows = gates.tile([P, B_TILES, H], BF16)
-                    nc.sync.dma_start(out=z_rows[:], in_=z.rearrange("(t p) n -> p t n", p=P))
-                if not last_chunk:
+                    w_in = [load_weight_chunk(nc, w_stream, W_in_words, g) for g in groups[::W_CHUNK]]
+                    if first == X_GROUPS // 4:
+                        r_rows = gates.tile([P, B_TILES, H], BF16)
+                        nc.sync.dma_start(out=r_rows[:], in_=r.rearrange("(t p) n -> p t n", p=P))
+                        z_rows = gates.tile([P, B_TILES, H], BF16)
+                        nc.sync.dma_start(out=z_rows[:], in_=z.rearrange("(t p) n -> p t n", p=P))
                     next_codes, next_planes = quantise_rows(x_chunk[:], X_CHUNK)
-                for g in range(first, first + X_CHUNK):
-                    multiply_group(
-                        nc, acc_i, codes, planes, g - first, w_in[(g - first) // W_CHUNK][:, g % W_CHUNK, :],
-                        w_planes[4 * (g % PLANES_PER_SLOT) : P, g // PLANES_PER_SLOT, :],
-                        start=(g == 0), stop=(g == X_GROUPS - 1),
-                    )
-                codes, planes = next_codes, next_planes
+                    for g in groups:
+                        multiply_group(
+                            nc, acc_i, codes, planes, g - first, w_in[(g - first) // W_CHUNK][:, g % W_CHUNK, :],
+                            w_plane[g], start=(g == 0), stop=False,
+                        )
+                    codes, planes = next_codes, next_planes
+                else:
+                    for c in range(N_HALVES):
+                        w_cols = slice(PACK * N_BANK * c, PACK * N_BANK * (c + 1))
+                        for pair in groups[::W_CHUNK]:
+                            w_half = w_stream.tile([P, W_CHUNK, PACK * N_BANK], U8, tag="half", align_bytes=64, bufs=4)
+                            nc.sync.dma_start(
+                                out=w_half[:].bitcast(I32),
+                                in_=W_in_words[pair : pair + W_CHUNK].rearrange("g p n t -> p g (n t)")[:, :, w_cols]
+                                .bitcast(I32),
+                            )
+                            for t in range(B_TILES):
+                                for g in range(pair, pair + W_CHUNK):
+                                    multiply(
+                                        nc, acc_i[t][c], codes, planes, g - first, t, w_half[:, g - pair, :],
+                                        w_plane[g][:, N_BANK * c : N_BANK * (c + 1)],
+                                        start=False, stop=(g == X_GROUPS - 1),
+                                    )
+                        for t in range(B_TILES):
+                            add_bias(nc, norms[t], c, acc_i[t][c], biases[:, 0:H])
+                            square_half(nc, work, norms[t], c)
+                if first == 0:
+                    for t in range(B_TILES):
+                        for c in range(N_HALVES):
+                            square_half(nc, work, norms_h[t], c)
+                        finish_norm(nc, norms_h[t], neg_half)
+                        make_shift(nc, norms_h[t])
                 if first == X_GROUPS // 2:
                     r_hn = gates.tile([P, B_TILES, H], F32)
                     one_minus_z = gates.tile([P, B_TILES, H], F32)
                     z_h = gates.tile([P, B_TILES, H], F32)
                     for t in range(B_TILES):
-                        nc.vector.tensor_mul(out=r_hn[:, t, :], in0=r_rows[:, t, :], in1=h_n[t][:])
-                        nc.vector.tensor_scalar(
-                            out=one_minus_z[:, t, :], in0=z_rows[:, t, :], scalar1=-1.0, scalar2=1.0,
-                            op0=ALU.mult, op1=ALU.add,
+                        v_h = norms_h[t]["v"]
+                        nc.scalar.activation(
+                            out=v_h[:], in_=v_h[:], func=ACT.Identity,
+                            bias=norms_h[t]["shift"][:], scale=norms_h[t]["rstd"][:],
+                        )
+                        nc.scalar.activation(
+                            out=one_minus_z[:, t, :], in_=z_rows[:, t, :], func=ACT.Copy, bias=1.0, scale=-1.0
                         )
                         nc.vector.tensor_mul(out=z_h[:, t, :], in0=z_rows[:, t, :], in1=h_rows[:, t, :])
+                        nc.vector.tensor_mul(out=r_hn[:, t, :], in0=r_rows[:, t, :], in1=v_h[:])
 
-        measured = [add_bias_and_measure(nc, work, small, acc_i[t], biases[:, 0:H], neg_half) for t in range(B_TILES)]
-        for t in range(B_TILES):
-            state, neg_mean, rstd = measured[t]
-            shift = small.tile([P, 1], F32, tag="shift")
-            nc.gpsimd.tensor_tensor(out=shift[:], in0=neg_mean[:], in1=rstd[:], op=ALU.mult)
-            halves = [slice(N_BANK * c, N_BANK * (c + 1)) for c in range(N_HALVES)]
-            for cols in halves:
+            def add_r_hn(t, c):
+                state, cols = norms[t]["v"], slice(N_BANK * c, N_BANK * (c + 1))
                 nc.vector.scalar_tensor_tensor(
-                    out=state[:, cols], in0=state[:, cols], scalar=rstd[:], in1=r_hn[:, t, cols],
+                    out=state[:, cols], in0=state[:, cols], scalar=norms[t]["rstd"][:], in1=r_hn[:, t, cols],
                     op0=ALU.mult, op1=ALU.add,
                 )
-                nc.scalar.activation(out=state[:, cols], in_=state[:, cols], func=ACT.Tanh, bias=shift[:], scale=1.0)
-            for cols in halves:
+                if c == 0:
+                    make_shift(nc, norms[t])
+                nc.scalar.activation(
+                    out=state[:, cols], in_=state[:, cols], func=ACT.Tanh, bias=norms[t]["shift"][:], scale=1.0
+                )
+
+            def gate(t, c):
+                state, cols = norms[t]["v"], slice(N_BANK * c, N_BANK * (c + 1))
                 nc.vector.tensor_mul(out=state[:, cols], in0=state[:, cols], in1=one_minus_z[:, t, cols])
-            for cols in halves:
+
+            def add_and_store(t, c):
+                state, cols = norms[t]["v"], slice(N_BANK * c, N_BANK * (c + 1))
                 nc.vector.tensor_add(out=state[:, cols], in0=state[:, cols], in1=z_h[:, t, cols])
                 nc.sync.dma_start(out=out[P * t : P * (t + 1), cols], in_=state[:, cols])
+
+            for t in range(B_TILES):
+                finish_norm(nc, norms[t], neg_half)
+            add_r_hn(0, 0)
+            add_r_hn(0, 1)
+            add_r_hn(1, 0)
+            gate(0, 0)
+            gate(0, 1)
+            add_r_hn(1, 1)
+            add_and_store(0, 0)
+            add_and_store(0, 1)
+            gate(1, 0)
+            add_and_store(1, 0)
+            gate(1, 1)
+            add_and_store(1, 1)

@@ -19,7 +19,6 @@ FLOPS = 2 * B * (I + H) * H
 P = 128
 PACK = 4
 K_GROUP = P * PACK
-PAIRS = K_GROUP // 2
 B_TILES = B // P
 N_BANK = 512
 N_HALVES = H // N_BANK
@@ -29,8 +28,8 @@ X_CHUNK = 4
 W_CHUNK = 2
 PLANES_PER_SLOT = 4
 IN_SLOTS = X_GROUPS // PLANES_PER_SLOT
-X_BUFS = 3
-W_BUFS = 11
+X_BUFS = 2
+W_BUFS = 10
 
 
 def load_weight_chunk(nc, stream, words, first_group):
@@ -62,14 +61,18 @@ def load_scale_planes(nc, planes, scales):
 
 
 def transpose_and_quantise(nc, psum, stage, identity, rows, n_groups, codes, planes):
-    words = rows.bitcast(F32)
+    ordered = stage.tile([P, B_TILES * X_CHUNK, 2, P], F32, tag="ordered", align_bytes=64)
+    nc.vector.tensor_copy(
+        out=ordered[:, : B_TILES * n_groups],
+        in_=rows.bitcast(F32).rearrange("p t (g w u) -> p (t g) u w", w=P, u=2),
+    )
     grouped = stage.tile([P, X_CHUNK * B_TILES * P * PACK], BF16, tag="grouped", align_bytes=64)
     grouped_words = grouped[:].bitcast(F32).rearrange("p (g t b u) -> p g t b u", g=X_CHUNK, t=B_TILES, u=2)
     for g in range(n_groups):
         bank = psum.tile([P, B_TILES, 2, P], F32, tag="bank")
         for t in range(B_TILES):
             for u in range(2):
-                nc.tensor.transpose(bank[:, t, u, :], words[:, t, PAIRS * g + u : PAIRS * (g + 1) : 2], identity[:])
+                nc.tensor.transpose(bank[:, t, u, :], ordered[:, n_groups * t + g, u, :], identity[:])
         side_by_side = bank[:].rearrange("p t u b -> p t b u")
         if g % 4 == 0:
             nc.vector.tensor_copy(out=grouped_words[:, g], in_=side_by_side)
@@ -173,7 +176,7 @@ def tile_layernormgrucell_pb_k_kernel(
         x_stream = stack.enter_context(tc.tile_pool(name="x_stream", bufs=X_BUFS))
         w_stream = stack.enter_context(tc.tile_pool(name="w_stream", bufs=W_BUFS))
         stage = stack.enter_context(tc.tile_pool(name="stage", bufs=2))
-        quantised = stack.enter_context(tc.tile_pool(name="quantised", bufs=3))
+        quantised = stack.enter_context(tc.tile_pool(name="quantised", bufs=2))
         gates = stack.enter_context(tc.tile_pool(name="gates", bufs=1))
         work = stack.enter_context(tc.tile_pool(name="work", bufs=2 * B_TILES))
         small = stack.enter_context(tc.tile_pool(name="small", bufs=2 * B_TILES))

@@ -24,7 +24,8 @@ N_BANK = 512
 N_HALVES = H // N_BANK
 X_GROUPS = I // K_GROUP
 H_GROUPS = H // K_GROUP
-X_CHUNK = 4
+X_CHUNKS = 8
+X_CHUNK = X_GROUPS // X_CHUNKS
 W_CHUNK = 2
 PLANES_PER_SLOT = 4
 IN_SLOTS = X_GROUPS // PLANES_PER_SLOT
@@ -60,12 +61,16 @@ def load_scale_planes(nc, planes, scales):
                 )
 
 
-def transpose_and_quantise(nc, psum, stage, identity, rows, n_groups, codes, planes):
+def order_words(nc, stage, rows, n_groups):
     ordered = stage.tile([P, B_TILES * X_CHUNK, 2, P], F32, tag="ordered", align_bytes=64)
     nc.vector.tensor_copy(
         out=ordered[:, : B_TILES * n_groups],
         in_=rows.bitcast(F32).rearrange("p t (g w u) -> p (t g) u w", w=P, u=2),
     )
+    return ordered
+
+
+def transpose_words(nc, psum, stage, identity, ordered, n_groups):
     grouped = stage.tile([P, X_CHUNK * B_TILES * P * PACK], BF16, tag="grouped", align_bytes=64)
     grouped_words = grouped[:].bitcast(F32).rearrange("p (g t b u) -> p g t b u", g=X_CHUNK, t=B_TILES, u=2)
     for g in range(n_groups):
@@ -73,16 +78,19 @@ def transpose_and_quantise(nc, psum, stage, identity, rows, n_groups, codes, pla
         for t in range(B_TILES):
             for u in range(2):
                 nc.tensor.transpose(bank[:, t, u, :], ordered[:, n_groups * t + g, u, :], identity[:])
-        side_by_side = bank[:].rearrange("p t u b -> p t b u")
-        if g % 4 == 0:
-            nc.vector.tensor_copy(out=grouped_words[:, g], in_=side_by_side)
-        else:
-            nc.scalar.copy(out=grouped_words[:, g], in_=side_by_side)
+        nc.scalar.copy(out=grouped_words[:, g], in_=bank[:].rearrange("p t u b -> p t b u"))
+    return grouped
+
+
+def quantise(nc, quantised, grouped, n_groups):
+    codes = quantised.tile([P, X_CHUNK, B_TILES, P], U32, tag="codes", align_bytes=64)
+    planes = quantised.tile([P, X_CHUNK, B_TILES, P], U8, tag="planes", align_bytes=64)
     nc.vector.quantize_mx(
-        out=codes.bitcast(FP8X4),
-        scales=planes,
+        out=codes[:, :n_groups].rearrange("p g t b -> p (g t b)").bitcast(FP8X4),
+        scales=planes[:, :n_groups].rearrange("p g t b -> p (g t b)"),
         in_=grouped[:, : n_groups * B_TILES * P * PACK],
     )
+    return codes, planes
 
 
 def multiply(nc, acc_half, codes, planes, g, t, w_words, w_plane, start, stop):
@@ -185,31 +193,21 @@ def tile_layernormgrucell_pb_k_kernel(
 
         identity = consts.tile([P, P], F32)
         make_identity(nc, identity[:])
+        neg_half = consts.tile([P, 1], F32)
+        nc.gpsimd.memset(neg_half[:], -0.5)
         bias_rows = consts.tile([P, 2 * H], BF16)
         nc.vector.memset(bias_rows[:].bitcast(I32), 0)
         w_planes = consts.tile([P, IN_SLOTS + 1, H], U8, align_bytes=64)
-        nc.vector.memset(w_planes[:].rearrange("p s n -> p (s n)").bitcast(I32), 0)
+        nc.gpsimd.memset(w_planes[:].rearrange("p s n -> p (s n)").bitcast(I32), 0)
         ones = consts.tile([P, P], BF16)
         nc.vector.memset(ones[:], 1.0)
-        neg_half = consts.tile([P, 1], F32)
-        nc.gpsimd.memset(neg_half[:], -0.5)
 
-        x_rows = x.rearrange("(t p) k -> p t k", p=P)
+        x_rows = x.rearrange("(p t) k -> p t k", t=B_TILES)
 
         def load_x(first):
             x_chunk = x_stream.tile([P, B_TILES, X_CHUNK * K_GROUP], BF16, tag="chunk", align_bytes=64)
             nc.sync.dma_start(out=x_chunk[:], in_=x_rows[:, :, K_GROUP * first : K_GROUP * (first + X_CHUNK)])
             return x_chunk
-
-        def quantise_rows(rows, n_groups):
-            codes = quantised.tile([P, X_CHUNK, B_TILES, P], U32, tag="codes", align_bytes=64)
-            planes = quantised.tile([P, X_CHUNK, B_TILES, P], U8, tag="planes", align_bytes=64)
-            transpose_and_quantise(
-                nc, psum, stage, identity, rows, n_groups,
-                codes[:, :n_groups].rearrange("p g t b -> p (g t b)"),
-                planes[:, :n_groups].rearrange("p g t b -> p (g t b)"),
-            )
-            return codes, planes
 
         def open_sums(kind):
             return [[sums_psum.tile([P, N_BANK], F32, tag="sums%d%d" % (t, c), name="%s%d%d" % (kind, t, c))
@@ -217,23 +215,31 @@ def tile_layernormgrucell_pb_k_kernel(
 
         with tc.manual_schedule():
             h_rows = gates.tile([P, B_TILES, H], BF16)
-            nc.sync.dma_start(out=h_rows[:], in_=h.rearrange("(t p) k -> p t k", p=P))
+            nc.sync.dma_start(out=h_rows[:], in_=h.rearrange("(p t) k -> p t k", t=B_TILES))
             x_chunk = load_x(0)
             nc.sync.dma_start(out=bias_rows[0:1, 0:H], in_=b_in.unsqueeze(0))
             nc.sync.dma_start(out=bias_rows[0:1, H : 2 * H], in_=b_hn.unsqueeze(0))
-            h_codes, h_planes = quantise_rows(h_rows[:], H_GROUPS)
+            h_grouped = transpose_words(
+                nc, psum, stage, identity, order_words(nc, stage, h_rows[:], H_GROUPS), H_GROUPS
+            )
+            ordered = order_words(nc, stage, x_chunk[:], X_CHUNK)
+            h_codes, h_planes = quantise(nc, quantised, h_grouped, H_GROUPS)
 
             w_hn = load_weight_chunk(nc, w_stream, W_hn_words, 0)
             load_scale_planes(nc, w_planes[:, IN_SLOTS : IN_SLOTS + 1, :], W_hn_scales)
             load_scale_planes(nc, w_planes[:, 0:IN_SLOTS, :], W_in_scales)
-            codes, planes = quantise_rows(x_chunk[:], X_CHUNK)
+            x_chunk = load_x(X_CHUNK)
+            w_next = [load_weight_chunk(nc, w_stream, W_in_words, g) for g in range(0, X_CHUNK, W_CHUNK)]
+            grouped = transpose_words(nc, psum, stage, identity, ordered, X_CHUNK)
 
             biases = consts.tile([P, 2 * H], BF16)
             for j in range(2 * N_HALVES):
                 cols = slice(N_BANK * j, N_BANK * (j + 1))
                 spread = psum.tile([P, N_BANK], F32, tag="bank")
                 nc.tensor.matmul(out=spread[:], lhsT=ones[:], rhs=bias_rows[:, cols], start=True, stop=True)
-                nc.vector.tensor_copy(out=biases[:, cols], in_=spread[:])
+                nc.scalar.copy(out=biases[:, cols], in_=spread[:])
+            codes, planes = quantise(nc, quantised, grouped, X_CHUNK)
+            ordered = order_words(nc, stage, x_chunk[:], X_CHUNK)
 
             acc_h = open_sums("acc_h")
             for g in range(H_GROUPS):
@@ -248,18 +254,40 @@ def tile_layernormgrucell_pb_k_kernel(
 
             acc_i = open_sums("acc_i")
             norms = [new_norm(work, small, "i%d" % t) for t in range(B_TILES)]
-            for first in range(0, X_GROUPS, X_CHUNK):
+            r_hn = gates.tile([P, B_TILES, H], F32)
+            one_minus_z = gates.tile([P, B_TILES, H], F32)
+            z_h = gates.tile([P, B_TILES, H], F32)
+
+            def prepare_gates(t):
+                v_h = norms_h[t]["v"]
+                nc.scalar.activation(
+                    out=v_h[:], in_=v_h[:], func=ACT.Identity,
+                    bias=norms_h[t]["shift"][:], scale=norms_h[t]["rstd"][:],
+                )
+                nc.scalar.activation(
+                    out=one_minus_z[:, t, :], in_=z_rows[:, t, :], func=ACT.Copy, bias=1.0, scale=-1.0
+                )
+                nc.vector.tensor_mul(out=z_h[:, t, :], in0=z_rows[:, t, :], in1=h_rows[:, t, :])
+                nc.vector.tensor_mul(out=r_hn[:, t, :], in0=r_rows[:, t, :], in1=v_h[:])
+
+            for chunk in range(X_CHUNKS):
+                first = X_CHUNK * chunk
                 groups = range(first, first + X_CHUNK)
                 w_plane = {g: w_planes[4 * (g % PLANES_PER_SLOT) : P, g // PLANES_PER_SLOT, :] for g in groups}
-                if first + X_CHUNK < X_GROUPS:
-                    x_chunk = load_x(first + X_CHUNK)
-                    w_in = [load_weight_chunk(nc, w_stream, W_in_words, g) for g in groups[::W_CHUNK]]
-                    if first == X_GROUPS // 4:
-                        r_rows = gates.tile([P, B_TILES, H], BF16)
-                        nc.sync.dma_start(out=r_rows[:], in_=r.rearrange("(t p) n -> p t n", p=P))
-                        z_rows = gates.tile([P, B_TILES, H], BF16)
-                        nc.sync.dma_start(out=z_rows[:], in_=z.rearrange("(t p) n -> p t n", p=P))
-                    next_codes, next_planes = quantise_rows(x_chunk[:], X_CHUNK)
+                w_in = w_next
+                if chunk + 2 < X_CHUNKS:
+                    x_chunk = load_x(first + 2 * X_CHUNK)
+                    w_next = [load_weight_chunk(nc, w_stream, W_in_words, g + X_CHUNK) for g in groups[::W_CHUNK]]
+                if chunk == 1:
+                    r_rows = gates.tile([P, B_TILES, H], BF16)
+                    nc.sync.dma_start(out=r_rows[:], in_=r.rearrange("(p t) n -> p t n", t=B_TILES))
+                    z_rows = gates.tile([P, B_TILES, H], BF16)
+                    nc.sync.dma_start(out=z_rows[:], in_=z.rearrange("(p t) n -> p t n", t=B_TILES))
+                if chunk + 1 < X_CHUNKS:
+                    grouped = transpose_words(nc, psum, stage, identity, ordered, X_CHUNK)
+                    next_codes, next_planes = quantise(nc, quantised, grouped, X_CHUNK)
+                    if chunk + 2 < X_CHUNKS:
+                        ordered = order_words(nc, stage, x_chunk[:], X_CHUNK)
                     for g in groups:
                         multiply_group(
                             nc, acc_i, codes, planes, g - first, w_in[(g - first) // W_CHUNK][:, g % W_CHUNK, :],
@@ -286,27 +314,18 @@ def tile_layernormgrucell_pb_k_kernel(
                         for t in range(B_TILES):
                             add_bias(nc, norms[t], c, acc_i[t][c], biases[:, 0:H])
                             square_half(nc, work, norms[t], c)
-                if first == 0:
+                if chunk == 0:
                     for t in range(B_TILES):
                         for c in range(N_HALVES):
                             square_half(nc, work, norms_h[t], c)
+                if chunk == 1:
+                    for t in range(B_TILES):
                         finish_norm(nc, norms_h[t], neg_half)
                         make_shift(nc, norms_h[t])
-                if first == X_GROUPS // 2:
-                    r_hn = gates.tile([P, B_TILES, H], F32)
-                    one_minus_z = gates.tile([P, B_TILES, H], F32)
-                    z_h = gates.tile([P, B_TILES, H], F32)
-                    for t in range(B_TILES):
-                        v_h = norms_h[t]["v"]
-                        nc.scalar.activation(
-                            out=v_h[:], in_=v_h[:], func=ACT.Identity,
-                            bias=norms_h[t]["shift"][:], scale=norms_h[t]["rstd"][:],
-                        )
-                        nc.scalar.activation(
-                            out=one_minus_z[:, t, :], in_=z_rows[:, t, :], func=ACT.Copy, bias=1.0, scale=-1.0
-                        )
-                        nc.vector.tensor_mul(out=z_h[:, t, :], in0=z_rows[:, t, :], in1=h_rows[:, t, :])
-                        nc.vector.tensor_mul(out=r_hn[:, t, :], in0=r_rows[:, t, :], in1=v_h[:])
+                if chunk in (3, 4):
+                    prepare_gates(chunk - 3)
+
+            out_rows = out.rearrange("(p t) n -> p t n", t=B_TILES)
 
             def add_r_hn(t, c):
                 state, cols = norms[t]["v"], slice(N_BANK * c, N_BANK * (c + 1))
@@ -327,7 +346,7 @@ def tile_layernormgrucell_pb_k_kernel(
             def add_and_store(t, c):
                 state, cols = norms[t]["v"], slice(N_BANK * c, N_BANK * (c + 1))
                 nc.vector.tensor_add(out=state[:, cols], in0=state[:, cols], in1=z_h[:, t, cols])
-                nc.sync.dma_start(out=out[P * t : P * (t + 1), cols], in_=state[:, cols])
+                nc.sync.dma_start(out=out_rows[:, t, cols], in_=state[:, cols])
 
             for t in range(B_TILES):
                 finish_norm(nc, norms[t], neg_half)

@@ -26,19 +26,24 @@ X_GROUPS = I // K_GROUP
 H_GROUPS = H // K_GROUP
 X_CHUNKS = 8
 X_CHUNK = X_GROUPS // X_CHUNKS
-W_CHUNK = 2
+CHUNK_K = X_CHUNK * K_GROUP
 PLANES_PER_SLOT = 4
+GPSIMD_ROWS = 6
 IN_SLOTS = X_GROUPS // PLANES_PER_SLOT
 X_BUFS = 2
-W_BUFS = 10
+W_BUFS = 5
 
 
-def load_weight_chunk(nc, stream, words, first_group):
-    chunk = stream.tile([P, W_CHUNK, PACK * H], U8, tag="chunk", align_bytes=64)
-    nc.sync.dma_start(
-        out=chunk[:].bitcast(I32),
-        in_=words[first_group : first_group + W_CHUNK].rearrange("g p n t -> p g (n t)").bitcast(I32),
-    )
+def load_weight(nc, pool, tag, words, groups, cols, n_loads=2, **tile_options):
+    n_groups, n_cols = groups.stop - groups.start, cols.stop - cols.start
+    chunk = pool.tile([P, n_groups, PACK * n_cols], U8, tag=tag, align_bytes=64, **tile_options)
+    by_partition = words[groups].rearrange("g p n t -> p g (n t)")
+    per_load = n_groups // n_loads
+    for first in range(0, n_groups, per_load):
+        nc.sync.dma_start(
+            out=chunk[:, first : first + per_load, :].bitcast(I32),
+            in_=by_partition[:, first : first + per_load, PACK * cols.start : PACK * cols.stop].bitcast(I32),
+        )
     return chunk
 
 
@@ -55,18 +60,21 @@ def load_scale_planes(nc, planes, scales):
             )
         else:
             for row in range(4):
-                nc.sync.dma_start(
-                    out=planes[first + row : first + row + 4 * per_slot : 4, :, :].bitcast(I32),
-                    in_=by_row[4 * quadrant + row].bitcast(I32),
+                on_gpsimd = 4 * quadrant + row >= 16 - GPSIMD_ROWS
+                queue, word = (nc.gpsimd, F32) if on_gpsimd else (nc.sync, I32)
+                queue.dma_start(
+                    out=planes[first + row : first + row + 4 * per_slot : 4, :, :].bitcast(word),
+                    in_=by_row[4 * quadrant + row].bitcast(word),
                 )
 
 
 def order_words(nc, stage, rows, n_groups):
-    ordered = stage.tile([P, B_TILES * X_CHUNK, 2, P], F32, tag="ordered", align_bytes=64)
-    nc.vector.tensor_copy(
-        out=ordered[:, : B_TILES * n_groups],
-        in_=rows.bitcast(F32).rearrange("p t (g w u) -> p (t g) u w", w=P, u=2),
-    )
+    ordered = stage.tile([P, B_TILES, X_CHUNK, 2, P], F32, tag="ordered", align_bytes=64)
+    for t in range(B_TILES):
+        nc.vector.tensor_copy(
+            out=ordered[:, t, :n_groups],
+            in_=rows[:, t, :].bitcast(F32).rearrange("p (g w u) -> p g u w", w=P, u=2),
+        )
     return ordered
 
 
@@ -77,7 +85,7 @@ def transpose_words(nc, psum, stage, identity, ordered, n_groups):
         bank = psum.tile([P, B_TILES, 2, P], F32, tag="bank")
         for t in range(B_TILES):
             for u in range(2):
-                nc.tensor.transpose(bank[:, t, u, :], ordered[:, n_groups * t + g, u, :], identity[:])
+                nc.tensor.transpose(bank[:, t, u, :], ordered[:, t, g, u, :], identity[:])
         nc.scalar.copy(out=grouped_words[:, g], in_=bank[:].rearrange("p t u b -> p t b u"))
     return grouped
 
@@ -123,7 +131,8 @@ def new_norm(work, small, label):
         "gap_sq": small.tile([P, 1], F32, tag="gap_sq", name="gap_sq_" + label),
         "sum_sq": small.tile([P, N_HALVES], F32, tag="sum_sq", name="sum_sq_" + label),
         "neg_mean": small.tile([P, 1], F32, tag="neg_mean", name="neg_mean_" + label),
-        "mean_sq": small.tile([P, 1], F32, tag="mean_sq", name="mean_sq_" + label),
+        "part": small.tile([P, 1], F32, tag="part", name="part_" + label),
+        "base": small.tile([P, 1], F32, tag="base", name="base_" + label),
         "var_eps": small.tile([P, 1], F32, tag="var_eps", name="var_eps_" + label),
         "rstd": small.tile([P, 1], F32, tag="rstd", name="rstd_" + label),
         "shift": small.tile([P, 1], F32, tag="shift", name="shift_" + label),
@@ -159,14 +168,22 @@ def square_half(nc, work, norm, c):
         )
 
 
+def begin_variance(nc, norm):
+    nc.vector.tensor_scalar(
+        out=norm["part"][:], in0=norm["sum_sq"][:, 0:1], scalar1=1.0 / H, scalar2=EPS, op0=ALU.mult, op1=ALU.add
+    )
+
+
+def subtract_gap(nc, norm):
+    nc.vector.tensor_scalar(
+        out=norm["base"][:], in0=norm["gap_sq"][:], scalar1=-1.0, scalar2=norm["part"][:], op0=ALU.mult, op1=ALU.add
+    )
+
+
 def finish_norm(nc, norm, neg_half):
     nc.vector.tensor_scalar(
-        out=norm["mean_sq"][:], in0=norm["sum_sq"][:, 0:1], scalar1=norm["sum_sq"][:, 1:2], scalar2=1.0 / H,
-        op0=ALU.add, op1=ALU.mult,
-    )
-    nc.vector.tensor_scalar(
-        out=norm["var_eps"][:], in0=norm["mean_sq"][:], scalar1=norm["gap_sq"][:], scalar2=EPS,
-        op0=ALU.subtract, op1=ALU.add,
+        out=norm["var_eps"][:], in0=norm["sum_sq"][:, 1:2], scalar1=1.0 / H, scalar2=norm["base"][:],
+        op0=ALU.mult, op1=ALU.add,
     )
     nc.gpsimd.tensor_tensor(out=norm["rstd"][:], in0=norm["var_eps"][:], in1=neg_half[:], op=ALU.pow)
 
@@ -196,17 +213,19 @@ def tile_layernormgrucell_pb_k_kernel(
         neg_half = consts.tile([P, 1], F32)
         nc.gpsimd.memset(neg_half[:], -0.5)
         bias_rows = consts.tile([P, 2 * H], BF16)
-        nc.vector.memset(bias_rows[:].bitcast(I32), 0)
-        w_planes = consts.tile([P, IN_SLOTS + 1, H], U8, align_bytes=64)
-        nc.gpsimd.memset(w_planes[:].rearrange("p s n -> p (s n)").bitcast(I32), 0)
+        nc.gpsimd.memset(bias_rows[:].bitcast(I32), 0)
+        hn_planes = consts.tile([P, 1, H], U8, align_bytes=64)
+        nc.gpsimd.memset(hn_planes[:].rearrange("p s n -> p (s n)").bitcast(I32), 0)
+        in_planes = consts.tile([P, IN_SLOTS, H], U8, align_bytes=64)
+        nc.vector.memset(in_planes[:].rearrange("p s n -> p (s n)").bitcast(I32), 0)
         ones = consts.tile([P, P], BF16)
         nc.vector.memset(ones[:], 1.0)
 
         x_rows = x.rearrange("(p t) k -> p t k", t=B_TILES)
 
-        def load_x(first):
-            x_chunk = x_stream.tile([P, B_TILES, X_CHUNK * K_GROUP], BF16, tag="chunk", align_bytes=64)
-            nc.sync.dma_start(out=x_chunk[:], in_=x_rows[:, :, K_GROUP * first : K_GROUP * (first + X_CHUNK)])
+        def load_x(chunk):
+            x_chunk = x_stream.tile([P, B_TILES, CHUNK_K], BF16, tag="chunk", align_bytes=64)
+            nc.sync.dma_start(out=x_chunk[:], in_=x_rows[:, :, CHUNK_K * chunk : CHUNK_K * (chunk + 1)])
             return x_chunk
 
         def open_sums(kind):
@@ -216,20 +235,20 @@ def tile_layernormgrucell_pb_k_kernel(
         with tc.manual_schedule():
             h_rows = gates.tile([P, B_TILES, H], BF16)
             nc.sync.dma_start(out=h_rows[:], in_=h.rearrange("(p t) k -> p t k", t=B_TILES))
-            x_chunk = load_x(0)
+            x_next = load_x(0)
             nc.sync.dma_start(out=bias_rows[0:1, 0:H], in_=b_in.unsqueeze(0))
             nc.sync.dma_start(out=bias_rows[0:1, H : 2 * H], in_=b_hn.unsqueeze(0))
             h_grouped = transpose_words(
                 nc, psum, stage, identity, order_words(nc, stage, h_rows[:], H_GROUPS), H_GROUPS
             )
-            ordered = order_words(nc, stage, x_chunk[:], X_CHUNK)
+            ordered = order_words(nc, stage, x_next[:], X_CHUNK)
             h_codes, h_planes = quantise(nc, quantised, h_grouped, H_GROUPS)
 
-            w_hn = load_weight_chunk(nc, w_stream, W_hn_words, 0)
-            load_scale_planes(nc, w_planes[:, IN_SLOTS : IN_SLOTS + 1, :], W_hn_scales)
-            load_scale_planes(nc, w_planes[:, 0:IN_SLOTS, :], W_in_scales)
-            x_chunk = load_x(X_CHUNK)
-            w_next = [load_weight_chunk(nc, w_stream, W_in_words, g) for g in range(0, X_CHUNK, W_CHUNK)]
+            load_scale_planes(nc, hn_planes[:], W_hn_scales)
+            w_hn = load_weight(nc, w_stream, "first_and_last", W_hn_words, slice(0, H_GROUPS), slice(0, H), n_loads=1, bufs=1)
+            load_scale_planes(nc, in_planes[:], W_in_scales)
+            x_next = load_x(1)
+            w_next = load_weight(nc, w_stream, "w_in", W_in_words, slice(0, X_CHUNK), slice(0, H))
             grouped = transpose_words(nc, psum, stage, identity, ordered, X_CHUNK)
 
             biases = consts.tile([P, 2 * H], BF16)
@@ -239,18 +258,18 @@ def tile_layernormgrucell_pb_k_kernel(
                 nc.tensor.matmul(out=spread[:], lhsT=ones[:], rhs=bias_rows[:, cols], start=True, stop=True)
                 nc.scalar.copy(out=biases[:, cols], in_=spread[:])
             codes, planes = quantise(nc, quantised, grouped, X_CHUNK)
-            ordered = order_words(nc, stage, x_chunk[:], X_CHUNK)
 
             acc_h = open_sums("acc_h")
             for g in range(H_GROUPS):
                 multiply_group(
-                    nc, acc_h, h_codes, h_planes, g, w_hn[:, g, :], w_planes[4 * g : P, IN_SLOTS, :],
+                    nc, acc_h, h_codes, h_planes, g, w_hn[:, g, :], hn_planes[4 * g : P, 0, :],
                     start=(g == 0), stop=(g == H_GROUPS - 1),
                 )
             norms_h = [new_norm(work, small, "h%d" % t) for t in range(B_TILES)]
             for t in range(B_TILES):
                 for c in range(N_HALVES):
                     add_bias(nc, norms_h[t], c, acc_h[t][c], biases[:, H : 2 * H])
+            ordered = order_words(nc, stage, x_next[:], X_CHUNK)
 
             acc_i = open_sums("acc_i")
             norms = [new_norm(work, small, "i%d" % t) for t in range(B_TILES)]
@@ -273,11 +292,12 @@ def tile_layernormgrucell_pb_k_kernel(
             for chunk in range(X_CHUNKS):
                 first = X_CHUNK * chunk
                 groups = range(first, first + X_CHUNK)
-                w_plane = {g: w_planes[4 * (g % PLANES_PER_SLOT) : P, g // PLANES_PER_SLOT, :] for g in groups}
+                w_plane = {g: in_planes[4 * (g % PLANES_PER_SLOT) : P, g // PLANES_PER_SLOT, :] for g in groups}
                 w_in = w_next
                 if chunk + 2 < X_CHUNKS:
-                    x_chunk = load_x(first + 2 * X_CHUNK)
-                    w_next = [load_weight_chunk(nc, w_stream, W_in_words, g + X_CHUNK) for g in groups[::W_CHUNK]]
+                    x_next = load_x(chunk + 2)
+                    following = slice(first + X_CHUNK, first + 2 * X_CHUNK)
+                    w_next = load_weight(nc, w_stream, "w_in", W_in_words, following, slice(0, H))
                 if chunk == 1:
                     r_rows = gates.tile([P, B_TILES, H], BF16)
                     nc.sync.dma_start(out=r_rows[:], in_=r.rearrange("(p t) n -> p t n", t=B_TILES))
@@ -287,39 +307,41 @@ def tile_layernormgrucell_pb_k_kernel(
                     grouped = transpose_words(nc, psum, stage, identity, ordered, X_CHUNK)
                     next_codes, next_planes = quantise(nc, quantised, grouped, X_CHUNK)
                     if chunk + 2 < X_CHUNKS:
-                        ordered = order_words(nc, stage, x_chunk[:], X_CHUNK)
+                        ordered = order_words(nc, stage, x_next[:], X_CHUNK)
                     for g in groups:
                         multiply_group(
-                            nc, acc_i, codes, planes, g - first, w_in[(g - first) // W_CHUNK][:, g % W_CHUNK, :],
+                            nc, acc_i, codes, planes, g - first, w_in[:, g - first, :],
                             w_plane[g], start=(g == 0), stop=False,
                         )
                     codes, planes = next_codes, next_planes
                 else:
                     for c in range(N_HALVES):
-                        w_cols = slice(PACK * N_BANK * c, PACK * N_BANK * (c + 1))
-                        for pair in groups[::W_CHUNK]:
-                            w_half = w_stream.tile([P, W_CHUNK, PACK * N_BANK], U8, tag="half", align_bytes=64, bufs=4)
-                            nc.sync.dma_start(
-                                out=w_half[:].bitcast(I32),
-                                in_=W_in_words[pair : pair + W_CHUNK].rearrange("g p n t -> p g (n t)")[:, :, w_cols]
-                                .bitcast(I32),
-                            )
+                        cols = slice(N_BANK * c, N_BANK * (c + 1))
+                        w_half = load_weight(
+                            nc, w_stream, ("first_and_last", "last")[c], W_in_words, slice(first, X_GROUPS), cols,
+                            bufs=1,
+                        )
+                        for pair in (groups[:2], groups[2:]):
                             for t in range(B_TILES):
-                                for g in range(pair, pair + W_CHUNK):
+                                for g in pair:
                                     multiply(
-                                        nc, acc_i[t][c], codes, planes, g - first, t, w_half[:, g - pair, :],
-                                        w_plane[g][:, N_BANK * c : N_BANK * (c + 1)],
-                                        start=False, stop=(g == X_GROUPS - 1),
+                                        nc, acc_i[t][c], codes, planes, g - first, t, w_half[:, g - first, :],
+                                        w_plane[g][:, cols], start=False, stop=(g == X_GROUPS - 1),
                                     )
                         for t in range(B_TILES):
                             add_bias(nc, norms[t], c, acc_i[t][c], biases[:, 0:H])
                             square_half(nc, work, norms[t], c)
+                        if c == 0:
+                            for t in range(B_TILES):
+                                begin_variance(nc, norms[t])
                 if chunk == 0:
                     for t in range(B_TILES):
                         for c in range(N_HALVES):
                             square_half(nc, work, norms_h[t], c)
                 if chunk == 1:
                     for t in range(B_TILES):
+                        begin_variance(nc, norms_h[t])
+                        subtract_gap(nc, norms_h[t])
                         finish_norm(nc, norms_h[t], neg_half)
                         make_shift(nc, norms_h[t])
                 if chunk in (3, 4):
@@ -348,6 +370,8 @@ def tile_layernormgrucell_pb_k_kernel(
                 nc.vector.tensor_add(out=state[:, cols], in0=state[:, cols], in1=z_h[:, t, cols])
                 nc.sync.dma_start(out=out_rows[:, t, cols], in_=state[:, cols])
 
+            for t in range(B_TILES):
+                subtract_gap(nc, norms[t])
             for t in range(B_TILES):
                 finish_norm(nc, norms[t], neg_half)
             add_r_hn(0, 0)

from contextlib import ExitStack

import concourse.mybir as mybir
from concourse.masks import make_identity

F32 = mybir.dt.float32
BF16 = mybir.dt.bfloat16
I32 = mybir.dt.int32
U32 = mybir.dt.uint32
U8 = mybir.dt.uint8
FP8X4 = mybir.dt.float8_e4m3fn_x4
ALU = mybir.AluOpType
ACT = mybir.ActivationFunctionType

B, I, H = 256, 16384, 1024
EPS = 1e-5
FLOPS = 2 * B * (I + H) * H

P = 128
PACK = 4
K_GROUP = P * PACK
B_TILES = B // P
N_BANK = 512
N_HALVES = H // N_BANK
X_GROUPS = I // K_GROUP
H_GROUPS = H // K_GROUP
X_CHUNKS = 8
X_CHUNK = X_GROUPS // X_CHUNKS
CHUNK_K = X_CHUNK * K_GROUP
PLANES_PER_SLOT = 4
GPSIMD_ROWS = 6
IN_SLOTS = X_GROUPS // PLANES_PER_SLOT
X_BUFS = 2
W_BUFS = 5


def load_weight(nc, pool, tag, words, groups, cols, n_loads=2, **tile_options):
    n_groups, n_cols = groups.stop - groups.start, cols.stop - cols.start
    chunk = pool.tile([P, n_groups, PACK * n_cols], U8, tag=tag, align_bytes=64, **tile_options)
    by_partition = words[groups].rearrange("g p n t -> p g (n t)")
    per_load = n_groups // n_loads
    for first in range(0, n_groups, per_load):
        nc.sync.dma_start(
            out=chunk[:, first : first + per_load, :].bitcast(I32),
            in_=by_partition[:, first : first + per_load, PACK * cols.start : PACK * cols.stop].bitcast(I32),
        )
    return chunk


def load_scale_planes(nc, planes, scales):
    n_slots = planes.shape[1]
    per_slot = scales.shape[0] // n_slots
    by_row = scales.rearrange("(s j) q n -> q j s n", j=per_slot)
    for quadrant in range(4):
        first = 32 * quadrant
        if n_slots == 1:
            nc.sync.dma_start(
                out=planes[first : first + 4 * per_slot, 0, :].bitcast(I32),
                in_=scales[:, 4 * quadrant : 4 * quadrant + 4, :].bitcast(I32),
            )
        else:
            for row in range(4):
                on_gpsimd = 4 * quadrant + row >= 16 - GPSIMD_ROWS
                queue, word = (nc.gpsimd, F32) if on_gpsimd else (nc.sync, I32)
                queue.dma_start(
                    out=planes[first + row : first + row + 4 * per_slot : 4, :, :].bitcast(word),
                    in_=by_row[4 * quadrant + row].bitcast(word),
                )


def order_words(nc, stage, rows, n_groups):
    ordered = stage.tile([P, B_TILES, X_CHUNK, 2, P], F32, tag="ordered", align_bytes=64)
    for t in range(B_TILES):
        nc.vector.tensor_copy(
            out=ordered[:, t, :n_groups],
            in_=rows[:, t, :].bitcast(F32).rearrange("p (g w u) -> p g u w", w=P, u=2),
        )
    return ordered


def transpose_words(nc, psum, stage, identity, ordered, n_groups):
    grouped = stage.tile([P, X_CHUNK * B_TILES * P * PACK], BF16, tag="grouped", align_bytes=64)
    grouped_words = grouped[:].bitcast(F32).rearrange("p (g t b u) -> p g t b u", g=X_CHUNK, t=B_TILES, u=2)
    for g in range(n_groups):
        bank = psum.tile([P, B_TILES, 2, P], F32, tag="bank")
        for t in range(B_TILES):
            for u in range(2):
                nc.tensor.transpose(bank[:, t, u, :], ordered[:, t, g, u, :], identity[:])
        nc.scalar.copy(out=grouped_words[:, g], in_=bank[:].rearrange("p t u b -> p t b u"))
    return grouped


def quantise(nc, quantised, grouped, n_groups):
    codes = quantised.tile([P, X_CHUNK, B_TILES, P], U32, tag="codes", align_bytes=64)
    planes = quantised.tile([P, X_CHUNK, B_TILES, P], U8, tag="planes", align_bytes=64)
    nc.vector.quantize_mx(
        out=codes[:, :n_groups].rearrange("p g t b -> p (g t b)").bitcast(FP8X4),
        scales=planes[:, :n_groups].rearrange("p g t b -> p (g t b)"),
        in_=grouped[:, : n_groups * B_TILES * P * PACK],
    )
    return codes, planes


def multiply(nc, acc_half, codes, planes, g, t, w_words, w_plane, start, stop):
    nc.tensor.matmul_mx(
        out=acc_half[:],
        lhsT=codes[:, g, t, :].bitcast(FP8X4),
        lhsT_scale=planes[:, g, t, :],
        rhs=w_words.bitcast(FP8X4),
        rhs_scale=w_plane,
        start=start,
        stop=stop,
    )


def multiply_group(nc, acc, codes, planes, g, w_words, w_plane, start, stop):
    for t in range(B_TILES):
        for c in range(N_HALVES):
            multiply(
                nc, acc[t][c], codes, planes, g, t, w_words[:, PACK * N_BANK * c : PACK * N_BANK * (c + 1)],
                w_plane[:, N_BANK * c : N_BANK * (c + 1)], start, stop,
            )


def new_norm(work, small, label):
    return {
        "v": work.tile([P, H], F32, tag="v", name="v_" + label),
        "sums": small.tile([P, N_HALVES], F32, tag="sums", name="sums_" + label),
        "neg_half_mean": small.tile([P, 1], F32, tag="neg_half_mean", name="neg_half_mean_" + label),
        "centre": small.tile([P, 1], F32, tag="centre", name="centre_" + label),
        "gap_sq": small.tile([P, 1], F32, tag="gap_sq", name="gap_sq_" + label),
        "sum_sq": small.tile([P, N_HALVES], F32, tag="sum_sq", name="sum_sq_" + label),
        "neg_mean": small.tile([P, 1], F32, tag="neg_mean", name="neg_mean_" + label),
        "part": small.tile([P, 1], F32, tag="part", name="part_" + label),
        "base": small.tile([P, 1], F32, tag="base", name="base_" + label),
        "var_eps": small.tile([P, 1], F32, tag="var_eps", name="var_eps_" + label),
        "rstd": small.tile([P, 1], F32, tag="rstd", name="rstd_" + label),
        "shift": small.tile([P, 1], F32, tag="shift", name="shift_" + label),
    }


def add_bias(nc, norm, c, acc_half, bias):
    cols = slice(N_BANK * c, N_BANK * (c + 1))
    nc.vector.scalar_tensor_tensor(
        out=norm["v"][:, cols], in0=acc_half[:], scalar=1.0, in1=bias[:, cols],
        op0=ALU.mult, op1=ALU.add, accum_out=norm["sums"][:, c : c + 1],
    )


def square_half(nc, work, norm, c):
    cols = slice(N_BANK * c, N_BANK * (c + 1))
    total = norm["sums"][:, c : c + 1]
    if c == 0:
        nc.scalar.activation(out=norm["centre"][:], in_=total, func=ACT.Copy, scale=-2.0 / H)
        nc.scalar.activation(out=norm["neg_half_mean"][:], in_=total, func=ACT.Copy, scale=-1.0 / H)
    else:
        nc.scalar.activation(
            out=norm["gap_sq"][:], in_=total, func=ACT.Square, bias=norm["neg_half_mean"][:], scale=1.0 / H
        )
    squares = work.tile([P, N_BANK], BF16, tag="squares", bufs=2)
    nc.scalar.activation(
        out=squares[:], in_=norm["v"][:, cols], func=ACT.Square, bias=norm["centre"][:], scale=1.0,
        accum_out=norm["sum_sq"][:, c : c + 1],
    )
    if c == 1:
        nc.scalar.activation(
            out=norm["neg_mean"][:], in_=total, func=ACT.Identity, bias=norm["neg_half_mean"][:], scale=-1.0 / H
        )


def begin_variance(nc, norm):
    nc.vector.tensor_scalar(
        out=norm["part"][:], in0=norm["sum_sq"][:, 0:1], scalar1=1.0 / H, scalar2=EPS, op0=ALU.mult, op1=ALU.add
    )


def subtract_gap(nc, norm):
    nc.vector.tensor_scalar(
        out=norm["base"][:], in0=norm["gap_sq"][:], scalar1=-1.0, scalar2=norm["part"][:], op0=ALU.mult, op1=ALU.add
    )


def finish_norm(nc, norm, neg_half):
    nc.vector.tensor_scalar(
        out=norm["var_eps"][:], in0=norm["sum_sq"][:, 1:2], scalar1=1.0 / H, scalar2=norm["base"][:],
        op0=ALU.mult, op1=ALU.add,
    )
    nc.gpsimd.tensor_tensor(out=norm["rstd"][:], in0=norm["var_eps"][:], in1=neg_half[:], op=ALU.pow)


def make_shift(nc, norm):
    nc.scalar.activation(out=norm["shift"][:], in_=norm["neg_mean"][:], func=ACT.Copy, scale=norm["rstd"][:])


def tile_layernormgrucell_pb_k_kernel(
    tc, x, h, r, z, W_in_words, W_in_scales, b_in, W_hn_words, W_hn_scales, b_hn, out
):
    nc = tc.nc
    with ExitStack() as stack:
        consts = stack.enter_context(tc.tile_pool(name="consts", bufs=1))
        x_stream = stack.enter_context(tc.tile_pool(name="x_stream", bufs=X_BUFS))
        w_stream = stack.enter_context(tc.tile_pool(name="w_stream", bufs=W_BUFS))
        stage = stack.enter_context(tc.tile_pool(name="stage", bufs=2))
        quantised = stack.enter_context(tc.tile_pool(name="quantised", bufs=2))
        gates = stack.enter_context(tc.tile_pool(name="gates", bufs=1))
        work = stack.enter_context(tc.tile_pool(name="work", bufs=2 * B_TILES))
        small = stack.enter_context(tc.tile_pool(name="small", bufs=2 * B_TILES))
        psum = stack.enter_context(tc.psum_pool(name="psum", bufs=4))
        sums_psum = stack.enter_context(tc.psum_pool(name="sums_psum", bufs=1))

        identity = consts.tile([P, P], F32)
        make_identity(nc, identity[:])
        neg_half = consts.tile([P, 1], F32)
        nc.gpsimd.memset(neg_half[:], -0.5)
        bias_rows = consts.tile([P, 2 * H], BF16)
        nc.gpsimd.memset(bias_rows[:].bitcast(I32), 0)
        hn_planes = consts.tile([P, 1, H], U8, align_bytes=64)
        nc.gpsimd.memset(hn_planes[:].rearrange("p s n -> p (s n)").bitcast(I32), 0)
        in_planes = consts.tile([P, IN_SLOTS, H], U8, align_bytes=64)
        nc.vector.memset(in_planes[:].rearrange("p s n -> p (s n)").bitcast(I32), 0)
        ones = consts.tile([P, P], BF16)
        nc.vector.memset(ones[:], 1.0)

        x_rows = x.rearrange("(p t) k -> p t k", t=B_TILES)

        def load_x(chunk):
            x_chunk = x_stream.tile([P, B_TILES, CHUNK_K], BF16, tag="chunk", align_bytes=64)
            nc.sync.dma_start(out=x_chunk[:], in_=x_rows[:, :, CHUNK_K * chunk : CHUNK_K * (chunk + 1)])
            return x_chunk

        def open_sums(kind):
            return [[sums_psum.tile([P, N_BANK], F32, tag="sums%d%d" % (t, c), name="%s%d%d" % (kind, t, c))
                     for c in range(N_HALVES)] for t in range(B_TILES)]

        with tc.manual_schedule():
            h_rows = gates.tile([P, B_TILES, H], BF16)
            nc.sync.dma_start(out=h_rows[:], in_=h.rearrange("(p t) k -> p t k", t=B_TILES))
            x_next = load_x(0)
            nc.sync.dma_start(out=bias_rows[0:1, 0:H], in_=b_in.unsqueeze(0))
            nc.sync.dma_start(out=bias_rows[0:1, H : 2 * H], in_=b_hn.unsqueeze(0))
            h_grouped = transpose_words(
                nc, psum, stage, identity, order_words(nc, stage, h_rows[:], H_GROUPS), H_GROUPS
            )
            ordered = order_words(nc, stage, x_next[:], X_CHUNK)
            h_codes, h_planes = quantise(nc, quantised, h_grouped, H_GROUPS)

            load_scale_planes(nc, hn_planes[:], W_hn_scales)
            w_hn = load_weight(nc, w_stream, "first_and_last", W_hn_words, slice(0, H_GROUPS), slice(0, H), n_loads=1, bufs=1)
            load_scale_planes(nc, in_planes[:], W_in_scales)
            x_next = load_x(1)
            w_next = load_weight(nc, w_stream, "w_in", W_in_words, slice(0, X_CHUNK), slice(0, H))
            grouped = transpose_words(nc, psum, stage, identity, ordered, X_CHUNK)

            biases = consts.tile([P, 2 * H], BF16)
            for j in range(2 * N_HALVES):
                cols = slice(N_BANK * j, N_BANK * (j + 1))
                spread = psum.tile([P, N_BANK], F32, tag="bank")
                nc.tensor.matmul(out=spread[:], lhsT=ones[:], rhs=bias_rows[:, cols], start=True, stop=True)
                nc.scalar.copy(out=biases[:, cols], in_=spread[:])
            codes, planes = quantise(nc, quantised, grouped, X_CHUNK)

            acc_h = open_sums("acc_h")
            for g in range(H_GROUPS):
                multiply_group(
                    nc, acc_h, h_codes, h_planes, g, w_hn[:, g, :], hn_planes[4 * g : P, 0, :],
                    start=(g == 0), stop=(g == H_GROUPS - 1),
                )
            norms_h = [new_norm(work, small, "h%d" % t) for t in range(B_TILES)]
            for t in range(B_TILES):
                for c in range(N_HALVES):
                    add_bias(nc, norms_h[t], c, acc_h[t][c], biases[:, H : 2 * H])
            ordered = order_words(nc, stage, x_next[:], X_CHUNK)

            acc_i = open_sums("acc_i")
            norms = [new_norm(work, small, "i%d" % t) for t in range(B_TILES)]
            r_hn = gates.tile([P, B_TILES, H], F32)
            one_minus_z = gates.tile([P, B_TILES, H], F32)
            z_h = gates.tile([P, B_TILES, H], F32)

            def prepare_gates(t):
                v_h = norms_h[t]["v"]
                nc.scalar.activation(
                    out=v_h[:], in_=v_h[:], func=ACT.Identity,
                    bias=norms_h[t]["shift"][:], scale=norms_h[t]["rstd"][:],
                )
                nc.scalar.activation(
                    out=one_minus_z[:, t, :], in_=z_rows[:, t, :], func=ACT.Copy, bias=1.0, scale=-1.0
                )
                nc.vector.tensor_mul(out=z_h[:, t, :], in0=z_rows[:, t, :], in1=h_rows[:, t, :])
                nc.vector.tensor_mul(out=r_hn[:, t, :], in0=r_rows[:, t, :], in1=v_h[:])

            for chunk in range(X_CHUNKS):
                first = X_CHUNK * chunk
                groups = range(first, first + X_CHUNK)
                w_plane = {g: in_planes[4 * (g % PLANES_PER_SLOT) : P, g // PLANES_PER_SLOT, :] for g in groups}
                w_in = w_next
                if chunk + 2 < X_CHUNKS:
                    x_next = load_x(chunk + 2)
                    following = slice(first + X_CHUNK, first + 2 * X_CHUNK)
                    w_next = load_weight(nc, w_stream, "w_in", W_in_words, following, slice(0, H))
                if chunk == 1:
                    r_rows = gates.tile([P, B_TILES, H], BF16)
                    nc.sync.dma_start(out=r_rows[:], in_=r.rearrange("(p t) n -> p t n", t=B_TILES))
                    z_rows = gates.tile([P, B_TILES, H], BF16)
                    nc.sync.dma_start(out=z_rows[:], in_=z.rearrange("(p t) n -> p t n", t=B_TILES))
                if chunk + 1 < X_CHUNKS:
                    grouped = transpose_words(nc, psum, stage, identity, ordered, X_CHUNK)
                    next_codes, next_planes = quantise(nc, quantised, grouped, X_CHUNK)
                    if chunk + 2 < X_CHUNKS:
                        ordered = order_words(nc, stage, x_next[:], X_CHUNK)
                    for g in groups:
                        multiply_group(
                            nc, acc_i, codes, planes, g - first, w_in[:, g - first, :],
                            w_plane[g], start=(g == 0), stop=False,
                        )
                    codes, planes = next_codes, next_planes
                else:
                    for c in range(N_HALVES):
                        cols = slice(N_BANK * c, N_BANK * (c + 1))
                        w_half = load_weight(
                            nc, w_stream, ("first_and_last", "last")[c], W_in_words, slice(first, X_GROUPS), cols,
                            bufs=1,
                        )
                        for pair in (groups[:2], groups[2:]):
                            for t in range(B_TILES):
                                for g in pair:
                                    multiply(
                                        nc, acc_i[t][c], codes, planes, g - first, t, w_half[:, g - first, :],
                                        w_plane[g][:, cols], start=False, stop=(g == X_GROUPS - 1),
                                    )
                        for t in range(B_TILES):
                            add_bias(nc, norms[t], c, acc_i[t][c], biases[:, 0:H])
                            square_half(nc, work, norms[t], c)
                        if c == 0:
                            for t in range(B_TILES):
                                begin_variance(nc, norms[t])
                if chunk == 0:
                    for t in range(B_TILES):
                        for c in range(N_HALVES):
                            square_half(nc, work, norms_h[t], c)
                if chunk == 1:
                    for t in range(B_TILES):
                        begin_variance(nc, norms_h[t])
                        subtract_gap(nc, norms_h[t])
                        finish_norm(nc, norms_h[t], neg_half)
                        make_shift(nc, norms_h[t])
                if chunk in (3, 4):
                    prepare_gates(chunk - 3)

            out_rows = out.rearrange("(p t) n -> p t n", t=B_TILES)

            def add_r_hn(t, c):
                state, cols = norms[t]["v"], slice(N_BANK * c, N_BANK * (c + 1))
                nc.vector.scalar_tensor_tensor(
                    out=state[:, cols], in0=state[:, cols], scalar=norms[t]["rstd"][:], in1=r_hn[:, t, cols],
                    op0=ALU.mult, op1=ALU.add,
                )
                if c == 0:
                    make_shift(nc, norms[t])
                nc.scalar.activation(
                    out=state[:, cols], in_=state[:, cols], func=ACT.Tanh, bias=norms[t]["shift"][:], scale=1.0
                )

            def gate(t, c):
                state, cols = norms[t]["v"], slice(N_BANK * c, N_BANK * (c + 1))
                nc.vector.tensor_mul(out=state[:, cols], in0=state[:, cols], in1=one_minus_z[:, t, cols])

            def add_and_store(t, c):
                state, cols = norms[t]["v"], slice(N_BANK * c, N_BANK * (c + 1))
                nc.vector.tensor_add(out=state[:, cols], in0=state[:, cols], in1=z_h[:, t, cols])
                nc.sync.dma_start(out=out_rows[:, t, cols], in_=state[:, cols])

            for t in range(B_TILES):
                subtract_gap(nc, norms[t])
            for t in range(B_TILES):
                finish_norm(nc, norms[t], neg_half)
            add_r_hn(0, 0)
            add_r_hn(0, 1)
            add_r_hn(1, 0)
            gate(0, 0)
            gate(0, 1)
            add_r_hn(1, 1)
            add_and_store(0, 0)
            add_and_store(0, 1)
            gate(1, 0)
            add_and_store(1, 0)
            gate(1, 1)
            add_and_store(1, 1)
